import numpy as np
import ml_dtypes


def mxq(x, axis, fmt="e4m3"):
    dtype, down = {"e4m3": (ml_dtypes.float8_e4m3fn, 7), "e5m2": (ml_dtypes.float8_e5m2, 14)}[fmt]
    v = np.moveaxis(np.asarray(x, np.float32).astype(ml_dtypes.bfloat16).astype(np.float64), axis, -1)
    blocks = v.reshape(v.shape[:-1] + (-1, 32))
    amax = np.abs(blocks).max(-1, keepdims=True)
    byte = np.maximum(np.where(amax > 0, np.frexp(amax)[1] - 1 + 127, 0) - down, 1)
    scale = np.exp2(byte - 127.0)
    codes = (blocks / scale).astype(np.float32).astype(dtype).astype(np.float64)
    return np.moveaxis((codes * scale).reshape(v.shape), -1, axis)


WIDE = False


def mx_kscale(k):
    if not WIDE:
        return np.ones(k)
    levels = np.array([10, -10, 5, -5, 0])
    if k % 512:
        return np.exp2(np.random.permutation(np.resize(levels, k // 32))).repeat(32)
    a = np.empty((k // 512, 16))
    for p in range(k // 512):
        a[p, :8] = np.random.permutation(np.resize(levels, 8))
        for g in range(8):
            far = levels[np.abs(levels - a[p, g]) >= 10]
            a[p, g + 8] = far[np.random.randint(len(far))]
    return np.exp2(a.ravel()).repeat(32)


BF16 = ml_dtypes.bfloat16


def bf(x):
    return np.asarray(x, np.float32).astype(BF16)


def f64(x):
    return np.asarray(x).astype(np.float64)


B, R, U, HID, G = 4096, 1024, 512, 1024, 256


def sigmoid(v):
    return 1.0 / (1.0 + np.exp(-v))


def setup_inputs():
    s = mx_kscale(R)
    return {"y_tilde": bf(np.random.standard_normal((B, R)) * s),
            "z_next": bf(np.random.standard_normal((B, R)) * s),
            "dt": bf(0.3 + 0.2 * np.random.random(1)),
            "glu_w1": bf(np.random.standard_normal((G, R)) * 1.5 / np.sqrt(R) / s),
            "glu_w2": bf(np.random.standard_normal((G, R)) / np.sqrt(R) / s),
            "glu_b1": bf(np.random.standard_normal(G) * 0.3),
            "glu_b2": bf(np.random.standard_normal(G) * 0.3)}


def reference(y_tilde, z_next, dt, glu_w1, glu_w2, glu_b1, glu_b2):
    y_next = f64(y_tilde) + f64(dt) * f64(z_next)
    yq = mxq(y_next, 1, "e4m3")
    gate = sigmoid((yq @ mxq(f64(glu_w1), 1, "e4m3").T) + f64(glu_b1))
    return gate * ((yq @ mxq(f64(glu_w2), 1, "e4m3").T) + f64(glu_b2))

@@ -1,0 +1,213 @@
+from contextlib import ExitStack
+
+import concourse.mybir as mybir
+from concourse.masks import make_identity
+
+BF16 = mybir.dt.bfloat16
+F32 = mybir.dt.float32
+U32 = mybir.dt.uint32
+U8 = mybir.dt.uint8
+FP8X4 = mybir.dt.float8_e4m3fn_x4
+ACT = mybir.ActivationFunctionType
+ALU = mybir.AluOpType
+
+P = 128
+ROWS, MODES, UNITS = 4096, 1024, 256
+K_PASS = 4 * P
+PASSES = MODES // K_PASS
+ROW_GROUPS = 4
+CHUNK_ROWS = P * ROW_GROUPS
+CHUNKS = ROWS // CHUNK_ROWS
+PAIRS = ROW_GROUPS // 2
+UNIT_TILES = UNITS // P
+CHUNKS_IN_SBUF = 4
+
+FLOPS = 2 * ROWS * MODES * 2 * UNITS
+
+
+def turn_and_group(nc, turned_pool, ident, row_words, grouped_words, pair):
+    columns = slice(2 * pair * P, 2 * (pair + 1) * P)
+    for g in range(PASSES):
+        turned = turned_pool.tile([P, 2, 2, P], F32, tag="turned")
+        for jj in range(2):
+            for u in range(2):
+                first_word = 2 * g * P
+                nc.tensor.transpose(
+                    turned[:, jj, u, :],
+                    row_words[:, 2 * pair + jj, first_word + u : first_word + 2 * P : 2],
+                    ident[:],
+                )
+        nc.scalar.copy(
+            out=grouped_words[:, g, columns, :].rearrange("p (j q) u -> p j q u", j=2),
+            in_=turned[:].rearrange("p j u q -> p j q u"),
+        )
+
+
+def quantise(nc, grouped, codes, scales):
+    nc.vector.quantize_mx(
+        out=codes[:].rearrange("p g c -> p (g c)").bitcast(FP8X4),
+        scales=scales[:].rearrange("p g c -> p (g c)"),
+        in_=grouped[:].rearrange("p g c t -> p (g c t)"),
+    )
+
+
+def tile_instrumentedlocmblock_pb_t_kernel(
+    tc, y_tilde, z_next, dt, glu_w1, glu_w2, glu_b1, glu_b2, out
+):
+    nc = tc.nc
+    y_chunks = y_tilde.rearrange("(c q j) k -> c q j k", q=P, j=ROW_GROUPS)
+    z_chunks = z_next.rearrange("(c q j) k -> c q j k", q=P, j=ROW_GROUPS)
+    out_chunks = out.rearrange("(c q j) n -> c q j n", q=P, j=ROW_GROUPS)
+
+    with ExitStack() as ctx:
+        const = ctx.enter_context(tc.tile_pool(name="const", bufs=1))
+        loads = ctx.enter_context(tc.tile_pool(name="loads", bufs=CHUNKS_IN_SBUF))
+        work = ctx.enter_context(tc.tile_pool(name="work", bufs=2))
+        turned_pool = ctx.enter_context(tc.psum_pool(name="turned", bufs=2))
+        sums_pool = ctx.enter_context(tc.psum_pool(name="sums", bufs=2 * UNIT_TILES))
+        back_pool = ctx.enter_context(tc.psum_pool(name="back", bufs=2))
+        ctx.enter_context(tc.manual_schedule())
+
+        loaded = {}
+        grouped_of = {}
+
+        def load(c):
+            y_rows = loads.tile([P, ROW_GROUPS, MODES], BF16)
+            z_rows = loads.tile([P, ROW_GROUPS, MODES], BF16)
+            for pair in range(PAIRS):
+                groups = slice(2 * pair, 2 * pair + 2)
+                nc.sync.dma_start(out=y_rows[:, groups, :], in_=y_chunks[c][:, groups, :])
+                nc.sync.dma_start(out=z_rows[:, groups, :], in_=z_chunks[c][:, groups, :])
+            loaded[c] = (y_rows, z_rows)
+
+        def add_and_turn(c):
+            y_rows, z_rows = loaded[c]
+            y_next = work.tile([P, ROW_GROUPS, MODES], BF16)
+            grouped = work.tile([P, PASSES, CHUNK_ROWS, 4], BF16, align_bytes=64, bufs=3)
+            for pair in range(PAIRS):
+                groups = slice(2 * pair, 2 * pair + 2)
+                nc.vector.scalar_tensor_tensor(
+                    out=y_next[:, groups, :],
+                    in0=z_rows[:, groups, :],
+                    scalar=dt_col[:, 0:1],
+                    in1=y_rows[:, groups, :],
+                    op0=ALU.mult,
+                    op1=ALU.add,
+                )
+                turn_and_group(
+                    nc, turned_pool, ident, y_next[:].bitcast(F32), grouped[:].bitcast(F32), pair
+                )
+            grouped_of[c] = grouped
+
+        def quantise_and_multiply(c):
+            y_codes = work.tile([P, PASSES, CHUNK_ROWS], U32, align_bytes=64)
+            y_scales = work.tile([P, PASSES, CHUNK_ROWS], U8, align_bytes=64)
+            quantise(nc, grouped_of[c], y_codes, y_scales)
+            halves = []
+            for h in range(UNIT_TILES):
+                gate_sum = sums_pool.tile([P, CHUNK_ROWS], F32, tag="sum")
+                value_sum = sums_pool.tile([P, CHUNK_ROWS], F32, tag="sum")
+                for acc, unit_tile in ((gate_sum, h), (value_sum, UNIT_TILES + h)):
+                    units = slice(unit_tile * P, (unit_tile + 1) * P)
+                    for g in range(PASSES):
+                        nc.tensor.matmul_mx(
+                            out=acc[:],
+                            lhsT=w_codes[:, g, units].bitcast(FP8X4),
+                            lhsT_scale=w_scales[:, g, units],
+                            rhs=y_codes[:, g, :].bitcast(FP8X4),
+                            rhs_scale=y_scales[:, g, :],
+                            start=(g == 0),
+                            stop=(g == PASSES - 1),
+                        )
+                gate = work.tile([P, CHUNK_ROWS], F32, bufs=2 * UNIT_TILES)
+                nc.scalar.activation(
+                    out=gate[:], in_=gate_sum[:], func=ACT.Sigmoid, bias=bias_col[:, h : h + 1], scale=1.0
+                )
+                halves.append((gate, value_sum))
+            return halves
+
+        def gate_and_store(c, halves):
+            product = work.tile([P, UNIT_TILES, CHUNK_ROWS], F32)
+            backs = [
+                back_pool.tile([P, 2, UNITS], F32, name="back%d" % pair, tag="back")
+                for pair in range(PAIRS)
+            ]
+            for h in range(UNIT_TILES):
+                gate, value_sum = halves[h]
+                nc.vector.scalar_tensor_tensor(
+                    out=product[:, h, :],
+                    in0=value_sum[:],
+                    scalar=bias_col[:, UNIT_TILES + h : UNIT_TILES + h + 1],
+                    in1=gate[:],
+                    op0=ALU.add,
+                    op1=ALU.mult,
+                )
+                for j in range(ROW_GROUPS):
+                    nc.tensor.transpose(
+                        backs[j // 2][:, j % 2, h * P : (h + 1) * P],
+                        product[:, h, j * P : (j + 1) * P],
+                        ident[:],
+                    )
+            result = work.tile([P, ROW_GROUPS, UNITS], F32)
+            for pair in range(PAIRS):
+                groups = slice(2 * pair, 2 * pair + 2)
+                nc.scalar.copy(out=result[:, groups, :], in_=backs[pair][:])
+                nc.sync.dma_start(out=out_chunks[c][:, groups, :], in_=result[:, groups, :])
+
+        ident = const.tile([P, P], F32)
+        make_identity(nc, ident[:])
+
+        dt_bf16 = const.tile([P, 1], BF16)
+        nc.scalar.dma_start(out=dt_bf16[:], in_=dt.partition_broadcast(P))
+        bias_bf16 = const.tile([2 * UNIT_TILES, P], BF16)
+        nc.scalar.dma_start(
+            out=bias_bf16[0:UNIT_TILES, :], in_=glu_b1.rearrange("(h n) -> h n", n=P)
+        )
+        nc.scalar.dma_start(
+            out=bias_bf16[UNIT_TILES : 2 * UNIT_TILES, :], in_=glu_b2.rearrange("(h n) -> h n", n=P)
+        )
+
+        load(0)
+        w_rows = const.tile([P, 2 * UNIT_TILES, MODES], BF16)
+        nc.sync.dma_start(
+            out=w_rows[:, 0:UNIT_TILES, :], in_=glu_w1.rearrange("(h q) k -> q h k", q=P)
+        )
+        nc.sync.dma_start(
+            out=w_rows[:, UNIT_TILES : 2 * UNIT_TILES, :], in_=glu_w2.rearrange("(h q) k -> q h k", q=P)
+        )
+        for c in range(1, CHUNKS_IN_SBUF):
+            load(c)
+
+        dt_col = const.tile([P, 1], F32)
+        nc.vector.tensor_copy(out=dt_col[:], in_=dt_bf16[:])
+
+        add_and_turn(0)
+
+        bias_rows = const.tile([P, P], F32)
+        nc.vector.memset(bias_rows[:], 0.0)
+        nc.vector.tensor_copy(out=bias_rows[0 : 2 * UNIT_TILES, :], in_=bias_bf16[:])
+        bias_turned = turned_pool.tile([P, 2, 2, P], F32, tag="turned")
+        nc.tensor.transpose(bias_turned[:, 0, 0, :], bias_rows[:], ident[:])
+        bias_col = const.tile([P, 2 * UNIT_TILES], F32)
+        nc.scalar.copy(out=bias_col[:], in_=bias_turned[:, 0, 0, 0 : 2 * UNIT_TILES])
+
+        w_grouped = work.tile([P, PASSES, CHUNK_ROWS, 4], BF16, align_bytes=64, tag="grouped", bufs=3)
+        for pair in range(PAIRS):
+            turn_and_group(
+                nc, turned_pool, ident, w_rows[:].bitcast(F32), w_grouped[:].bitcast(F32), pair
+            )
+        add_and_turn(1)
+        w_codes = const.tile([P, PASSES, CHUNK_ROWS], U32, align_bytes=64)
+        w_scales = const.tile([P, PASSES, CHUNK_ROWS], U8, align_bytes=64)
+        quantise(nc, w_grouped, w_codes, w_scales)
+
+        halves_of = {}
+        for c in range(CHUNKS + 1):
+            if c + CHUNKS_IN_SBUF < CHUNKS:
+                load(c + CHUNKS_IN_SBUF)
+            if c < CHUNKS:
+                halves_of[c] = quantise_and_multiply(c)
+            if c >= 1:
+                gate_and_store(c - 1, halves_of[c - 1])
+            if c + 2 < CHUNKS:
+                add_and_turn(c + 2)

@@ -16,6 +16,9 @@ ROWS, MODES, UNITS = 4096, 1024, 256
 K_PASS = 4 * P
 PASSES = MODES // K_PASS
 ROW_GROUPS = 4
+ADD_GROUPS = 3
+ADD_ROWS = ADD_GROUPS * P
+HALF = P // 2
 CHUNK_ROWS = P * ROW_GROUPS
 CHUNKS = ROWS // CHUNK_ROWS
 PAIRS = ROW_GROUPS // 2
@@ -25,22 +28,33 @@ CHUNKS_IN_SBUF = 4
 FLOPS = 2 * ROWS * MODES * 2 * UNITS
 
 
-def turn_and_group(nc, turned_pool, ident, row_words, grouped_words, pair):
-    columns = slice(2 * pair * P, 2 * (pair + 1) * P)
+def turn_and_group(nc, turned_pool, ident, words, grouped_words, group):
+    turned = turned_pool.tile([P, PASSES, 2, P], F32, tag="turned")
     for g in range(PASSES):
-        turned = turned_pool.tile([P, 2, 2, P], F32, tag="turned")
-        for jj in range(2):
-            for u in range(2):
-                first_word = 2 * g * P
-                nc.tensor.transpose(
-                    turned[:, jj, u, :],
-                    row_words[:, 2 * pair + jj, first_word + u : first_word + 2 * P : 2],
-                    ident[:],
+        for u in range(2):
+            nc.tensor.transpose(turned[:, g, u, :], words[g][u], ident[:])
+    nc.scalar.copy(
+        out=grouped_words[:, :, group * P : (group + 1) * P, :],
+        in_=turned[:].rearrange("p g u q -> p g q u"),
+    )
+
+
+def add_turned_and_group(nc, turned_pool, select, yz_rows, grouped):
+    added = turned_pool.tile([P, PASSES, 4, P], BF16, tag="turned")
+    for i in range(2):
+        for g in range(PASSES):
+            for t in range(4):
+                nc.tensor.matmul(
+                    out=added[:, g, t, i * HALF : (i + 1) * HALF],
+                    lhsT=yz_rows[:, i, g * K_PASS + t : (g + 1) * K_PASS : 4],
+                    rhs=select[:],
+                    start=True,
+                    stop=True,
                 )
-        nc.scalar.copy(
-            out=grouped_words[:, g, columns, :].rearrange("p (j q) u -> p j q u", j=2),
-            in_=turned[:].rearrange("p j u q -> p j q u"),
-        )
+    nc.scalar.copy(
+        out=grouped[:, :, ADD_GROUPS * P : CHUNK_ROWS, :],
+        in_=added[:].rearrange("p g t q -> p g q t"),
+    )
 
 
 def quantise(nc, grouped, codes, scales):
@@ -55,9 +69,10 @@ def tile_instrumentedlocmblock_pb_t_kernel(
     tc, y_tilde, z_next, dt, glu_w1, glu_w2, glu_b1, glu_b2, out
 ):
     nc = tc.nc
-    y_chunks = y_tilde.rearrange("(c q j) k -> c q j k", q=P, j=ROW_GROUPS)
-    z_chunks = z_next.rearrange("(c q j) k -> c q j k", q=P, j=ROW_GROUPS)
-    out_chunks = out.rearrange("(c q j) n -> c q j n", q=P, j=ROW_GROUPS)
+
+    def rows_of(tensor, c):
+        rows = tensor[c * CHUNK_ROWS : (c + 1) * CHUNK_ROWS, :]
+        return rows[0:ADD_ROWS, :].rearrange("(q j) k -> q j k", q=P), rows[ADD_ROWS:CHUNK_ROWS, :]
 
     with ExitStack() as ctx:
         const = ctx.enter_context(tc.tile_pool(name="const", bufs=1))
@@ -68,35 +83,56 @@ def tile_instrumentedlocmblock_pb_t_kernel(
         back_pool = ctx.enter_context(tc.psum_pool(name="back", bufs=2))
         ctx.enter_context(tc.manual_schedule())
 
+        def splits_of(c):
+            return [slice(0, 1), slice(1, ADD_GROUPS)] if c == 0 else [slice(0, ADD_GROUPS)]
+
         loaded = {}
         grouped_of = {}
 
         def load(c):
-            y_rows = loads.tile([P, ROW_GROUPS, MODES], BF16)
-            z_rows = loads.tile([P, ROW_GROUPS, MODES], BF16)
-            for pair in range(PAIRS):
-                groups = slice(2 * pair, 2 * pair + 2)
-                nc.sync.dma_start(out=y_rows[:, groups, :], in_=y_chunks[c][:, groups, :])
-                nc.sync.dma_start(out=z_rows[:, groups, :], in_=z_chunks[c][:, groups, :])
-            loaded[c] = (y_rows, z_rows)
+            y_rows = loads.tile([P, ADD_GROUPS, MODES], BF16)
+            z_rows = loads.tile([P, ADD_GROUPS, MODES], BF16)
+            yz_rows = loads.tile([P, 2, MODES], BF16)
+            y_dram, y_last = rows_of(y_tilde, c)
+            z_dram, z_last = rows_of(z_next, c)
+            for groups in splits_of(c):
+                nc.sync.dma_start(out=y_rows[:, groups, :], in_=y_dram[:, groups, :])
+                nc.sync.dma_start(out=z_rows[:, groups, :], in_=z_dram[:, groups, :])
+            nc.sync.dma_start(out=yz_rows[0:P:2, :, :], in_=y_last.rearrange("(i q) k -> q i k", q=HALF))
+            nc.sync.dma_start(out=yz_rows[1:P:2, :, :], in_=z_last.rearrange("(i q) k -> q i k", q=HALF))
+            loaded[c] = (y_rows, z_rows, yz_rows)
 
         def add_and_turn(c):
-            y_rows, z_rows = loaded[c]
-            y_next = work.tile([P, ROW_GROUPS, MODES], BF16)
+            y_rows, z_rows, yz_rows = loaded[c]
+            y_next = work.tile([P, ADD_GROUPS, 2, MODES // 2], BF16)
             grouped = work.tile([P, PASSES, CHUNK_ROWS, 4], BF16, align_bytes=64, bufs=3)
-            for pair in range(PAIRS):
-                groups = slice(2 * pair, 2 * pair + 2)
-                nc.vector.scalar_tensor_tensor(
-                    out=y_next[:, groups, :],
-                    in0=z_rows[:, groups, :],
-                    scalar=dt_col[:, 0:1],
-                    in1=y_rows[:, groups, :],
-                    op0=ALU.mult,
-                    op1=ALU.add,
-                )
-                turn_and_group(
-                    nc, turned_pool, ident, y_next[:].bitcast(F32), grouped[:].bitcast(F32), pair
-                )
+            add_turned_and_group(nc, turned_pool, select, yz_rows, grouped)
+            next_words = y_next[:].rearrange("q j u k -> q (j u k)").bitcast(F32)
+            for groups in splits_of(c):
+                for u in range(2):
+                    nc.vector.scalar_tensor_tensor(
+                        out=y_next[:, groups, u, :].rearrange("q j (w e) -> q j w e", e=2),
+                        in0=z_rows[:, groups, :].rearrange("q j (w u e) -> q u j w e", u=2, e=2)[:, u],
+                        scalar=dt_col[:, 0:1],
+                        in1=y_rows[:, groups, :].rearrange("q j (w u e) -> q u j w e", u=2, e=2)[:, u],
+                        op0=ALU.mult,
+                        op1=ALU.add,
+                    )
+                for group in range(groups.start, groups.stop):
+                    turn_and_group(
+                        nc,
+                        turned_pool,
+                        ident,
+                        [
+                            [
+                                next_words[:, ((2 * group + u) * PASSES + g) * P : ((2 * group + u) * PASSES + g + 1) * P]
+                                for u in range(2)
+                            ]
+                            for g in range(PASSES)
+                        ],
+                        grouped[:].bitcast(F32),
+                        group,
+                    )
             grouped_of[c] = grouped
 
         def quantise_and_multiply(c):
@@ -150,9 +186,10 @@ def tile_instrumentedlocmblock_pb_t_kernel(
                     )
             result = work.tile([P, ROW_GROUPS, UNITS], F32)
             for pair in range(PAIRS):
-                groups = slice(2 * pair, 2 * pair + 2)
-                nc.scalar.copy(out=result[:, groups, :], in_=backs[pair][:])
-                nc.sync.dma_start(out=out_chunks[c][:, groups, :], in_=result[:, groups, :])
+                nc.scalar.copy(out=result[:, 2 * pair : 2 * pair + 2, :], in_=backs[pair][:])
+            out_added, out_last = rows_of(out, c)
+            nc.sync.dma_start(out=out_added, in_=result[:, 0:ADD_GROUPS, :])
+            nc.sync.dma_start(out=out_last, in_=result[:, ADD_GROUPS, :])
 
         ident = const.tile([P, P], F32)
         make_identity(nc, ident[:])
@@ -180,6 +217,15 @@ def tile_instrumentedlocmblock_pb_t_kernel(
 
         dt_col = const.tile([P, 1], F32)
         nc.vector.tensor_copy(out=dt_col[:], in_=dt_bf16[:])
+        select = const.tile([P, HALF], BF16)
+        nc.vector.scalar_tensor_tensor(
+            out=select[:],
+            in0=ident[:, 1:P:2],
+            scalar=dt_col[:, 0:1],
+            in1=ident[:, 0:P:2],
+            op0=ALU.mult,
+            op1=ALU.add,
+        )
 
         add_and_turn(0)
 
@@ -192,9 +238,18 @@ def tile_instrumentedlocmblock_pb_t_kernel(
         nc.scalar.copy(out=bias_col[:], in_=bias_turned[:, 0, 0, 0 : 2 * UNIT_TILES])
 
         w_grouped = work.tile([P, PASSES, CHUNK_ROWS, 4], BF16, align_bytes=64, tag="grouped", bufs=3)
-        for pair in range(PAIRS):
+        w_words = w_rows[:].bitcast(F32)
+        for group in range(ROW_GROUPS):
             turn_and_group(
-                nc, turned_pool, ident, w_rows[:].bitcast(F32), w_grouped[:].bitcast(F32), pair
+                nc,
+                turned_pool,
+                ident,
+                [
+                    [w_words[:, group, 2 * g * P + u : 2 * (g + 1) * P : 2] for u in range(2)]
+                    for g in range(PASSES)
+                ],
+                w_grouped[:].bitcast(F32),
+                group,
             )
         add_and_turn(1)
         w_codes = const.tile([P, PASSES, CHUNK_ROWS], U32, align_bytes=64)

@@ -18,6 +18,7 @@ PASSES = MODES // K_PASS
 ROW_GROUPS = 4
 ADD_GROUPS = 3
 ADD_ROWS = ADD_GROUPS * P
+GROUP_ORDER = (ADD_GROUPS, 0, 1, 2)
 HALF = P // 2
 CHUNK_ROWS = P * ROW_GROUPS
 CHUNKS = ROWS // CHUNK_ROWS
@@ -87,7 +88,13 @@ def tile_instrumentedlocmblock_pb_t_kernel(
             return [slice(0, 1), slice(1, ADD_GROUPS)] if c == 0 else [slice(0, ADD_GROUPS)]
 
         loaded = {}
+        added = {}
         grouped_of = {}
+        quantised = {}
+        sums_of = {}
+        gates_of = {}
+        product_of = {}
+        result_of = {}
 
         def load(c):
             y_rows = loads.tile([P, ADD_GROUPS, MODES], BF16)
@@ -102,12 +109,9 @@ def tile_instrumentedlocmblock_pb_t_kernel(
             nc.sync.dma_start(out=yz_rows[1:P:2, :, :], in_=z_last.rearrange("(i q) k -> q i k", q=HALF))
             loaded[c] = (y_rows, z_rows, yz_rows)
 
-        def add_and_turn(c):
+        def add(c):
             y_rows, z_rows, yz_rows = loaded[c]
             y_next = work.tile([P, ADD_GROUPS, 2, MODES // 2], BF16)
-            grouped = work.tile([P, PASSES, CHUNK_ROWS, 4], BF16, align_bytes=64, bufs=3)
-            add_turned_and_group(nc, turned_pool, select, yz_rows, grouped)
-            next_words = y_next[:].rearrange("q j u k -> q (j u k)").bitcast(F32)
             for groups in splits_of(c):
                 for u in range(2):
                     nc.vector.scalar_tensor_tensor(
@@ -118,78 +122,93 @@ def tile_instrumentedlocmblock_pb_t_kernel(
                         op0=ALU.mult,
                         op1=ALU.add,
                     )
-                for group in range(groups.start, groups.stop):
-                    turn_and_group(
-                        nc,
-                        turned_pool,
-                        ident,
-                        [
-                            [
-                                next_words[:, ((2 * group + u) * PASSES + g) * P : ((2 * group + u) * PASSES + g + 1) * P]
-                                for u in range(2)
-                            ]
-                            for g in range(PASSES)
-                        ],
-                        grouped[:].bitcast(F32),
-                        group,
-                    )
-            grouped_of[c] = grouped
+            added[c] = (y_next, yz_rows)
 
-        def quantise_and_multiply(c):
+        def turn(c, group):
+            y_next, yz_rows = added[c]
+            if group == GROUP_ORDER[0]:
+                grouped_of[c] = work.tile([P, PASSES, CHUNK_ROWS, 4], BF16, name="grouped", align_bytes=64, bufs=3)
+            grouped = grouped_of[c]
+            if group == ADD_GROUPS:
+                add_turned_and_group(nc, turned_pool, select, yz_rows, grouped)
+                return
+            next_words = y_next[:].rearrange("q j u k -> q (j u k)").bitcast(F32)
+            turn_and_group(
+                nc,
+                turned_pool,
+                ident,
+                [
+                    [
+                        next_words[:, ((2 * group + u) * PASSES + g) * P : ((2 * group + u) * PASSES + g + 1) * P]
+                        for u in range(2)
+                    ]
+                    for g in range(PASSES)
+                ],
+                grouped[:].bitcast(F32),
+                group,
+            )
+
+        def quantise_chunk(c):
             y_codes = work.tile([P, PASSES, CHUNK_ROWS], U32, align_bytes=64)
             y_scales = work.tile([P, PASSES, CHUNK_ROWS], U8, align_bytes=64)
             quantise(nc, grouped_of[c], y_codes, y_scales)
-            halves = []
-            for h in range(UNIT_TILES):
-                gate_sum = sums_pool.tile([P, CHUNK_ROWS], F32, tag="sum")
-                value_sum = sums_pool.tile([P, CHUNK_ROWS], F32, tag="sum")
-                for acc, unit_tile in ((gate_sum, h), (value_sum, UNIT_TILES + h)):
-                    units = slice(unit_tile * P, (unit_tile + 1) * P)
-                    for g in range(PASSES):
-                        nc.tensor.matmul_mx(
-                            out=acc[:],
-                            lhsT=w_codes[:, g, units].bitcast(FP8X4),
-                            lhsT_scale=w_scales[:, g, units],
-                            rhs=y_codes[:, g, :].bitcast(FP8X4),
-                            rhs_scale=y_scales[:, g, :],
-                            start=(g == 0),
-                            stop=(g == PASSES - 1),
-                        )
+            quantised[c] = (y_codes, y_scales)
+            sums_of[c] = []
+            gates_of[c] = []
+
+        def multiply(c, s):
+            y_codes, y_scales = quantised[c]
+            acc = sums_pool.tile([P, CHUNK_ROWS], F32, name="acc", tag="sum")
+            unit_tile = UNIT_TILES * (s % 2) + s // 2
+            units = slice(unit_tile * P, (unit_tile + 1) * P)
+            for g in range(PASSES):
+                nc.tensor.matmul_mx(
+                    out=acc[:],
+                    lhsT=w_codes[:, g, units].bitcast(FP8X4),
+                    lhsT_scale=w_scales[:, g, units],
+                    rhs=y_codes[:, g, :].bitcast(FP8X4),
+                    rhs_scale=y_scales[:, g, :],
+                    start=(g == 0),
+                    stop=(g == PASSES - 1),
+                )
+            sums_of[c].append(acc)
+            if s % 2 == 0:
                 gate = work.tile([P, CHUNK_ROWS], F32, bufs=2 * UNIT_TILES)
                 nc.scalar.activation(
-                    out=gate[:], in_=gate_sum[:], func=ACT.Sigmoid, bias=bias_col[:, h : h + 1], scale=1.0
+                    out=gate[:], in_=acc[:], func=ACT.Sigmoid, bias=bias_col[:, s // 2 : s // 2 + 1], scale=1.0
                 )
-                halves.append((gate, value_sum))
-            return halves
+                gates_of[c].append(gate)
 
-        def gate_and_store(c, halves):
+        def gate_chunk(c):
             product = work.tile([P, UNIT_TILES, CHUNK_ROWS], F32)
-            backs = [
-                back_pool.tile([P, 2, UNITS], F32, name="back%d" % pair, tag="back")
-                for pair in range(PAIRS)
-            ]
             for h in range(UNIT_TILES):
-                gate, value_sum = halves[h]
                 nc.vector.scalar_tensor_tensor(
                     out=product[:, h, :],
-                    in0=value_sum[:],
+                    in0=sums_of[c][2 * h + 1][:],
                     scalar=bias_col[:, UNIT_TILES + h : UNIT_TILES + h + 1],
-                    in1=gate[:],
+                    in1=gates_of[c][h][:],
                     op0=ALU.add,
                     op1=ALU.mult,
                 )
-                for j in range(ROW_GROUPS):
+            product_of[c] = product
+            result_of[c] = work.tile([P, ROW_GROUPS, UNITS], F32, name="result")
+
+        def turn_back(c, pair):
+            back = back_pool.tile([P, 2, UNITS], F32, tag="back")
+            for jj in range(2):
+                j = 2 * pair + jj
+                for h in range(UNIT_TILES):
                     nc.tensor.transpose(
-                        backs[j // 2][:, j % 2, h * P : (h + 1) * P],
-                        product[:, h, j * P : (j + 1) * P],
+                        back[:, jj, h * P : (h + 1) * P],
+                        product_of[c][:, h, j * P : (j + 1) * P],
                         ident[:],
                     )
-            result = work.tile([P, ROW_GROUPS, UNITS], F32)
-            for pair in range(PAIRS):
-                nc.scalar.copy(out=result[:, 2 * pair : 2 * pair + 2, :], in_=backs[pair][:])
-            out_added, out_last = rows_of(out, c)
-            nc.sync.dma_start(out=out_added, in_=result[:, 0:ADD_GROUPS, :])
-            nc.sync.dma_start(out=out_last, in_=result[:, ADD_GROUPS, :])
+            result = result_of[c]
+            nc.scalar.copy(out=result[:, 2 * pair : 2 * pair + 2, :], in_=back[:])
+            if pair == PAIRS - 1:
+                out_added, out_last = rows_of(out, c)
+                nc.sync.dma_start(out=out_added, in_=result[:, 0:ADD_GROUPS, :])
+                nc.sync.dma_start(out=out_last, in_=result[:, ADD_GROUPS, :])
 
         ident = const.tile([P, P], F32)
         make_identity(nc, ident[:])
@@ -227,7 +246,9 @@ def tile_instrumentedlocmblock_pb_t_kernel(
             op1=ALU.add,
         )
 
-        add_and_turn(0)
+        add(0)
+        for group in GROUP_ORDER:
+            turn(0, group)
 
         bias_rows = const.tile([P, P], F32)
         nc.vector.memset(bias_rows[:], 0.0)
@@ -251,18 +272,24 @@ def tile_instrumentedlocmblock_pb_t_kernel(
                 w_grouped[:].bitcast(F32),
                 group,
             )
-        add_and_turn(1)
+        add(1)
         w_codes = const.tile([P, PASSES, CHUNK_ROWS], U32, align_bytes=64)
         w_scales = const.tile([P, PASSES, CHUNK_ROWS], U8, align_bytes=64)
         quantise(nc, w_grouped, w_codes, w_scales)
 
-        halves_of = {}
         for c in range(CHUNKS + 1):
             if c + CHUNKS_IN_SBUF < CHUNKS:
                 load(c + CHUNKS_IN_SBUF)
             if c < CHUNKS:
-                halves_of[c] = quantise_and_multiply(c)
+                quantise_chunk(c)
             if c >= 1:
-                gate_and_store(c - 1, halves_of[c - 1])
+                gate_chunk(c - 1)
+            for s in range(2 * UNIT_TILES):
+                if c + 1 < CHUNKS:
+                    turn(c + 1, GROUP_ORDER[s])
+                if c < CHUNKS:
+                    multiply(c, s)
+                if c >= 1 and s % 2 == 1:
+                    turn_back(c - 1, s // 2)
             if c + 2 < CHUNKS:
-                add_and_turn(c + 2)
+                add(c + 2)

@@ -284,12 +284,18 @@ def tile_instrumentedlocmblock_pb_t_kernel(
                 quantise_chunk(c)
             if c >= 1:
                 gate_chunk(c - 1)
-            for s in range(2 * UNIT_TILES):
-                if c + 1 < CHUNKS:
-                    turn(c + 1, GROUP_ORDER[s])
+            turned_groups = [GROUP_ORDER[:2], GROUP_ORDER[2:]]
+            for half in range(2):
+                if half == 0 and c + 1 < CHUNKS:
+                    for group in turned_groups[0]:
+                        turn(c + 1, group)
                 if c < CHUNKS:
-                    multiply(c, s)
-                if c >= 1 and s % 2 == 1:
-                    turn_back(c - 1, s // 2)
+                    multiply(c, 2 * half)
+                    multiply(c, 2 * half + 1)
+                if half == 0 and c + 1 < CHUNKS:
+                    for group in turned_groups[1]:
+                        turn(c + 1, group)
+                if c >= 1:
+                    turn_back(c - 1, half)
             if c + 2 < CHUNKS:
                 add(c + 2)

@@ -15,46 +15,49 @@ P = 128
 ROWS, MODES, UNITS = 4096, 1024, 256
 K_PASS = 4 * P
 PASSES = MODES // K_PASS
-ROW_GROUPS = 4
+UNIT_TILES = UNITS // P
+HALF = P // 2
+
+BLOCK_ROWS = 512
+BLOCKS = ROWS // BLOCK_ROWS
 ADD_GROUPS = 3
 ADD_ROWS = ADD_GROUPS * P
-GROUP_ORDER = (ADD_GROUPS, 0, 1, 2)
-HALF = P // 2
-CHUNK_ROWS = P * ROW_GROUPS
+BLOCKS_IN_SBUF = 4
+
+CHUNK_GROUPS = 2
+CHUNK_ROWS = CHUNK_GROUPS * P
 CHUNKS = ROWS // CHUNK_ROWS
-PAIRS = ROW_GROUPS // 2
-UNIT_TILES = UNITS // P
-CHUNKS_IN_SBUF = 4
+GROUPS_OF_CHUNK = ((ADD_GROUPS, 0), (1, 2))
 
 FLOPS = 2 * ROWS * MODES * 2 * UNITS
 
 
-def turn_and_group(nc, turned_pool, ident, words, grouped_words, group):
+def turn(nc, turned_pool, ident, words, grouped_words, columns):
     turned = turned_pool.tile([P, PASSES, 2, P], F32, tag="turned")
     for g in range(PASSES):
         for u in range(2):
             nc.tensor.transpose(turned[:, g, u, :], words[g][u], ident[:])
     nc.scalar.copy(
-        out=grouped_words[:, :, group * P : (group + 1) * P, :],
+        out=grouped_words[:, :, columns, :],
         in_=turned[:].rearrange("p g u q -> p g q u"),
     )
 
 
-def add_turned_and_group(nc, turned_pool, select, yz_rows, grouped):
-    added = turned_pool.tile([P, PASSES, 4, P], BF16, tag="turned")
+def add_and_turn(nc, turned_pool, select, yz_rows, grouped, columns):
+    turned = turned_pool.tile([P, PASSES, 4, P], BF16, tag="turned")
     for i in range(2):
         for g in range(PASSES):
             for t in range(4):
                 nc.tensor.matmul(
-                    out=added[:, g, t, i * HALF : (i + 1) * HALF],
+                    out=turned[:, g, t, i * HALF : (i + 1) * HALF],
                     lhsT=yz_rows[:, i, g * K_PASS + t : (g + 1) * K_PASS : 4],
                     rhs=select[:],
                     start=True,
                     stop=True,
                 )
     nc.scalar.copy(
-        out=grouped[:, :, ADD_GROUPS * P : CHUNK_ROWS, :],
-        in_=added[:].rearrange("p g t q -> p g q t"),
+        out=grouped[:, :, columns, :],
+        in_=turned[:].rearrange("p g t q -> p g q t"),
     )
 
 
@@ -71,21 +74,18 @@ def tile_instrumentedlocmblock_pb_t_kernel(
 ):
     nc = tc.nc
 
-    def rows_of(tensor, c):
-        rows = tensor[c * CHUNK_ROWS : (c + 1) * CHUNK_ROWS, :]
-        return rows[0:ADD_ROWS, :].rearrange("(q j) k -> q j k", q=P), rows[ADD_ROWS:CHUNK_ROWS, :]
+    def rows_of(tensor, b):
+        rows = tensor[b * BLOCK_ROWS : (b + 1) * BLOCK_ROWS, :]
+        return rows[0:ADD_ROWS, :].rearrange("(q j) k -> q j k", q=P), rows[ADD_ROWS:BLOCK_ROWS, :]
 
     with ExitStack() as ctx:
         const = ctx.enter_context(tc.tile_pool(name="const", bufs=1))
-        loads = ctx.enter_context(tc.tile_pool(name="loads", bufs=CHUNKS_IN_SBUF))
+        loads = ctx.enter_context(tc.tile_pool(name="loads", bufs=BLOCKS_IN_SBUF))
         work = ctx.enter_context(tc.tile_pool(name="work", bufs=2))
         turned_pool = ctx.enter_context(tc.psum_pool(name="turned", bufs=2))
         sums_pool = ctx.enter_context(tc.psum_pool(name="sums", bufs=2 * UNIT_TILES))
         back_pool = ctx.enter_context(tc.psum_pool(name="back", bufs=2))
         ctx.enter_context(tc.manual_schedule())
-
-        def splits_of(c):
-            return [slice(0, 1), slice(1, ADD_GROUPS)] if c == 0 else [slice(0, ADD_GROUPS)]
 
         loaded = {}
         added = {}
@@ -96,86 +96,100 @@ def tile_instrumentedlocmblock_pb_t_kernel(
         product_of = {}
         result_of = {}
 
-        def load(c):
-            y_rows = loads.tile([P, ADD_GROUPS, MODES], BF16)
-            z_rows = loads.tile([P, ADD_GROUPS, MODES], BF16)
-            yz_rows = loads.tile([P, 2, MODES], BF16)
-            y_dram, y_last = rows_of(y_tilde, c)
-            z_dram, z_last = rows_of(z_next, c)
-            for groups in splits_of(c):
-                nc.sync.dma_start(out=y_rows[:, groups, :], in_=y_dram[:, groups, :])
-                nc.sync.dma_start(out=z_rows[:, groups, :], in_=z_dram[:, groups, :])
-            nc.sync.dma_start(out=yz_rows[0:P:2, :, :], in_=y_last.rearrange("(i q) k -> q i k", q=HALF))
-            nc.sync.dma_start(out=yz_rows[1:P:2, :, :], in_=z_last.rearrange("(i q) k -> q i k", q=HALF))
-            loaded[c] = (y_rows, z_rows, yz_rows)
+        def add_groups(c):
+            groups = [group for group in GROUPS_OF_CHUNK[c % 2] if group < ADD_GROUPS]
+            return slice(groups[0], groups[-1] + 1)
 
-        def add(c):
-            y_rows, z_rows, yz_rows = loaded[c]
-            y_next = work.tile([P, ADD_GROUPS, 2, MODES // 2], BF16)
-            for groups in splits_of(c):
-                for u in range(2):
-                    nc.vector.scalar_tensor_tensor(
-                        out=y_next[:, groups, u, :].rearrange("q j (w e) -> q j w e", e=2),
-                        in0=z_rows[:, groups, :].rearrange("q j (w u e) -> q u j w e", u=2, e=2)[:, u],
-                        scalar=dt_col[:, 0:1],
-                        in1=y_rows[:, groups, :].rearrange("q j (w u e) -> q u j w e", u=2, e=2)[:, u],
-                        op0=ALU.mult,
-                        op1=ALU.add,
-                    )
-            added[c] = (y_next, yz_rows)
-
-        def turn(c, group):
-            y_next, yz_rows = added[c]
-            if group == GROUP_ORDER[0]:
-                grouped_of[c] = work.tile([P, PASSES, CHUNK_ROWS, 4], BF16, name="grouped", align_bytes=64, bufs=3)
-            grouped = grouped_of[c]
-            if group == ADD_GROUPS:
-                add_turned_and_group(nc, turned_pool, select, yz_rows, grouped)
-                return
-            next_words = y_next[:].rearrange("q j u k -> q (j u k)").bitcast(F32)
-            turn_and_group(
-                nc,
-                turned_pool,
-                ident,
-                [
-                    [
-                        next_words[:, ((2 * group + u) * PASSES + g) * P : ((2 * group + u) * PASSES + g + 1) * P]
-                        for u in range(2)
-                    ]
-                    for g in range(PASSES)
-                ],
-                grouped[:].bitcast(F32),
-                group,
+        def make_block(b):
+            loaded[b] = (
+                loads.tile([P, ADD_GROUPS, MODES], BF16, name="y_rows"),
+                loads.tile([P, ADD_GROUPS, MODES], BF16, name="z_rows"),
+                loads.tile([P, 2, MODES], BF16, name="yz_rows"),
             )
+
+        def load_added(b, groups):
+            for rows, tensor in zip(loaded[b], (y_tilde, z_next)):
+                nc.sync.dma_start(out=rows[:, groups, :], in_=rows_of(tensor, b)[0][:, groups, :])
+
+        def load_last(b):
+            for first, tensor in enumerate((y_tilde, z_next)):
+                nc.sync.dma_start(
+                    out=loaded[b][2][first:P:2, :, :],
+                    in_=rows_of(tensor, b)[1].rearrange("(i q) k -> q i k", q=HALF),
+                )
+
+        def load(b):
+            make_block(b)
+            load_added(b, slice(0, ADD_GROUPS))
+            load_last(b)
+
+        def add_chunk(c):
+            y_rows, z_rows = loaded[c // 2][:2]
+            groups = add_groups(c)
+            y_next = work.tile([P, CHUNK_GROUPS, 2, MODES // 2], BF16)
+            for u in range(2):
+                nc.vector.scalar_tensor_tensor(
+                    out=y_next[:, 0 : groups.stop - groups.start, u, :].rearrange("q j (w e) -> q j w e", e=2),
+                    in0=z_rows[:, groups, :].rearrange("q j (w u e) -> q u j w e", u=2, e=2)[:, u],
+                    scalar=dt_col[:, 0:1],
+                    in1=y_rows[:, groups, :].rearrange("q j (w u e) -> q u j w e", u=2, e=2)[:, u],
+                    op0=ALU.mult,
+                    op1=ALU.add,
+                )
+            added[c] = y_next
+
+        def turn_chunk(c):
+            grouped = work.tile([P, PASSES, CHUNK_ROWS, 4], BF16, align_bytes=64, bufs=3)
+            next_words = added[c][:].rearrange("q j u k -> q (j u k)").bitcast(F32)
+            for i, group in enumerate(GROUPS_OF_CHUNK[c % 2]):
+                columns = slice(i * P, (i + 1) * P)
+                if group == ADD_GROUPS:
+                    add_and_turn(nc, turned_pool, select, loaded[c // 2][2], grouped, columns)
+                else:
+                    j = group - add_groups(c).start
+                    first = [[((2 * j + u) * PASSES + g) * P for u in range(2)] for g in range(PASSES)]
+                    turn(
+                        nc,
+                        turned_pool,
+                        ident,
+                        [[next_words[:, word : word + P] for word in pair] for pair in first],
+                        grouped[:].bitcast(F32),
+                        columns,
+                    )
+            grouped_of[c] = grouped
 
         def quantise_chunk(c):
             y_codes = work.tile([P, PASSES, CHUNK_ROWS], U32, align_bytes=64)
             y_scales = work.tile([P, PASSES, CHUNK_ROWS], U8, align_bytes=64)
             quantise(nc, grouped_of[c], y_codes, y_scales)
             quantised[c] = (y_codes, y_scales)
+
+        def multiply_chunk(c):
+            y_codes, y_scales = quantised[c]
             sums_of[c] = []
             gates_of[c] = []
-
-        def multiply(c, s):
-            y_codes, y_scales = quantised[c]
-            acc = sums_pool.tile([P, CHUNK_ROWS], F32, name="acc", tag="sum")
-            unit_tile = UNIT_TILES * (s % 2) + s // 2
-            units = slice(unit_tile * P, (unit_tile + 1) * P)
-            for g in range(PASSES):
-                nc.tensor.matmul_mx(
-                    out=acc[:],
-                    lhsT=w_codes[:, g, units].bitcast(FP8X4),
-                    lhsT_scale=w_scales[:, g, units],
-                    rhs=y_codes[:, g, :].bitcast(FP8X4),
-                    rhs_scale=y_scales[:, g, :],
-                    start=(g == 0),
-                    stop=(g == PASSES - 1),
-                )
-            sums_of[c].append(acc)
-            if s % 2 == 0:
+            for h in range(UNIT_TILES):
+                for unit_tile in (h, UNIT_TILES + h):
+                    units = slice(unit_tile * P, (unit_tile + 1) * P)
+                    acc = sums_pool.tile([P, 2, CHUNK_ROWS], F32, name="acc", tag="sum")
+                    for g in range(PASSES):
+                        nc.tensor.matmul_mx(
+                            out=acc[:, 0, :],
+                            lhsT=w_codes[:, g, units].bitcast(FP8X4),
+                            lhsT_scale=w_scales[:, g, units],
+                            rhs=y_codes[:, g, :].bitcast(FP8X4),
+                            rhs_scale=y_scales[:, g, :],
+                            start=(g == 0),
+                            stop=(g == PASSES - 1),
+                        )
+                    sums_of[c].append(acc)
                 gate = work.tile([P, CHUNK_ROWS], F32, bufs=2 * UNIT_TILES)
                 nc.scalar.activation(
-                    out=gate[:], in_=acc[:], func=ACT.Sigmoid, bias=bias_col[:, s // 2 : s // 2 + 1], scale=1.0
+                    out=gate[:],
+                    in_=sums_of[c][2 * h][:, 0, :],
+                    func=ACT.Sigmoid,
+                    bias=bias_col[:, h : h + 1],
+                    scale=1.0,
                 )
                 gates_of[c].append(gate)
 
@@ -184,31 +198,34 @@ def tile_instrumentedlocmblock_pb_t_kernel(
             for h in range(UNIT_TILES):
                 nc.vector.scalar_tensor_tensor(
                     out=product[:, h, :],
-                    in0=sums_of[c][2 * h + 1][:],
+                    in0=sums_of[c][2 * h + 1][:, 0, :],
                     scalar=bias_col[:, UNIT_TILES + h : UNIT_TILES + h + 1],
                     in1=gates_of[c][h][:],
                     op0=ALU.add,
                     op1=ALU.mult,
                 )
             product_of[c] = product
-            result_of[c] = work.tile([P, ROW_GROUPS, UNITS], F32, name="result")
 
-        def turn_back(c, pair):
-            back = back_pool.tile([P, 2, UNITS], F32, tag="back")
-            for jj in range(2):
-                j = 2 * pair + jj
+        def turn_back_and_store(c):
+            b = c // 2
+            back = back_pool.tile([P, CHUNK_GROUPS, UNITS], F32, tag="back")
+            for i in range(CHUNK_GROUPS):
                 for h in range(UNIT_TILES):
                     nc.tensor.transpose(
-                        back[:, jj, h * P : (h + 1) * P],
-                        product_of[c][:, h, j * P : (j + 1) * P],
+                        back[:, i, h * P : (h + 1) * P],
+                        product_of[c][:, h, i * P : (i + 1) * P],
                         ident[:],
                     )
-            result = result_of[c]
-            nc.scalar.copy(out=result[:, 2 * pair : 2 * pair + 2, :], in_=back[:])
-            if pair == PAIRS - 1:
-                out_added, out_last = rows_of(out, c)
-                nc.sync.dma_start(out=out_added, in_=result[:, 0:ADD_GROUPS, :])
-                nc.sync.dma_start(out=out_last, in_=result[:, ADD_GROUPS, :])
+            if c % 2 == 0:
+                result_of[b] = work.tile([P, 1 + ADD_GROUPS, UNITS], F32, name="result", bufs=3)
+            result = result_of[b]
+            first = CHUNK_GROUPS * (c % 2)
+            nc.scalar.copy(out=result[:, first : first + CHUNK_GROUPS, :], in_=back[:])
+            out_added, out_last = rows_of(out, b)
+            if c % 2 == 0:
+                nc.sync.dma_start(out=out_last, in_=result[:, 0, :])
+            else:
+                nc.sync.dma_start(out=out_added, in_=result[:, 1 : 1 + ADD_GROUPS, :])
 
         ident = const.tile([P, P], F32)
         make_identity(nc, ident[:])
@@ -223,7 +240,9 @@ def tile_instrumentedlocmblock_pb_t_kernel(
             out=bias_bf16[UNIT_TILES : 2 * UNIT_TILES, :], in_=glu_b2.rearrange("(h n) -> h n", n=P)
         )
 
-        load(0)
+        make_block(0)
+        load_added(0, add_groups(0))
+        load_last(0)
         w_rows = const.tile([P, 2 * UNIT_TILES, MODES], BF16)
         nc.sync.dma_start(
             out=w_rows[:, 0:UNIT_TILES, :], in_=glu_w1.rearrange("(h q) k -> q h k", q=P)
@@ -231,8 +250,9 @@ def tile_instrumentedlocmblock_pb_t_kernel(
         nc.sync.dma_start(
             out=w_rows[:, UNIT_TILES : 2 * UNIT_TILES, :], in_=glu_w2.rearrange("(h q) k -> q h k", q=P)
         )
-        for c in range(1, CHUNKS_IN_SBUF):
-            load(c)
+        load_added(0, add_groups(1))
+        for b in range(1, BLOCKS_IN_SBUF):
+            load(b)
 
         dt_col = const.tile([P, 1], F32)
         nc.vector.tensor_copy(out=dt_col[:], in_=dt_bf16[:])
@@ -246,56 +266,48 @@ def tile_instrumentedlocmblock_pb_t_kernel(
             op1=ALU.add,
         )
 
-        add(0)
-        for group in GROUP_ORDER:
-            turn(0, group)
+        add_chunk(0)
+        turn_chunk(0)
 
         bias_rows = const.tile([P, P], F32)
         nc.vector.memset(bias_rows[:], 0.0)
         nc.vector.tensor_copy(out=bias_rows[0 : 2 * UNIT_TILES, :], in_=bias_bf16[:])
-        bias_turned = turned_pool.tile([P, 2, 2, P], F32, tag="turned")
+        bias_turned = turned_pool.tile([P, PASSES, 2, P], F32, tag="turned")
         nc.tensor.transpose(bias_turned[:, 0, 0, :], bias_rows[:], ident[:])
         bias_col = const.tile([P, 2 * UNIT_TILES], F32)
         nc.scalar.copy(out=bias_col[:], in_=bias_turned[:, 0, 0, 0 : 2 * UNIT_TILES])
 
-        w_grouped = work.tile([P, PASSES, CHUNK_ROWS, 4], BF16, align_bytes=64, tag="grouped", bufs=3)
+        add_chunk(1)
+        w_grouped = const.tile([P, PASSES, 2 * UNITS, 4], BF16, align_bytes=64)
         w_words = w_rows[:].bitcast(F32)
-        for group in range(ROW_GROUPS):
-            turn_and_group(
+        for tile_of_units in range(2 * UNIT_TILES):
+            turn(
                 nc,
                 turned_pool,
                 ident,
                 [
-                    [w_words[:, group, 2 * g * P + u : 2 * (g + 1) * P : 2] for u in range(2)]
+                    [w_words[:, tile_of_units, 2 * g * P + u : 2 * (g + 1) * P : 2] for u in range(2)]
                     for g in range(PASSES)
                 ],
                 w_grouped[:].bitcast(F32),
-                group,
+                slice(tile_of_units * P, (tile_of_units + 1) * P),
             )
-        add(1)
-        w_codes = const.tile([P, PASSES, CHUNK_ROWS], U32, align_bytes=64)
-        w_scales = const.tile([P, PASSES, CHUNK_ROWS], U8, align_bytes=64)
+        w_codes = const.tile([P, PASSES, 2 * UNITS], U32, align_bytes=64)
+        w_scales = const.tile([P, PASSES, 2 * UNITS], U8, align_bytes=64)
         quantise(nc, w_grouped, w_codes, w_scales)
 
         for c in range(CHUNKS + 1):
-            if c + CHUNKS_IN_SBUF < CHUNKS:
-                load(c + CHUNKS_IN_SBUF)
+            if c % 2 == 0 and c // 2 + BLOCKS_IN_SBUF < BLOCKS:
+                load(c // 2 + BLOCKS_IN_SBUF)
             if c < CHUNKS:
                 quantise_chunk(c)
             if c >= 1:
                 gate_chunk(c - 1)
-            turned_groups = [GROUP_ORDER[:2], GROUP_ORDER[2:]]
-            for half in range(2):
-                if half == 0 and c + 1 < CHUNKS:
-                    for group in turned_groups[0]:
-                        turn(c + 1, group)
-                if c < CHUNKS:
-                    multiply(c, 2 * half)
-                    multiply(c, 2 * half + 1)
-                if half == 0 and c + 1 < CHUNKS:
-                    for group in turned_groups[1]:
-                        turn(c + 1, group)
-                if c >= 1:
-                    turn_back(c - 1, half)
             if c + 2 < CHUNKS:
-                add(c + 2)
+                add_chunk(c + 2)
+            if c + 1 < CHUNKS:
+                turn_chunk(c + 1)
+            if c < CHUNKS:
+                multiply_chunk(c)
+            if c >= 1:
+                turn_back_and_store(c - 1)

@@ -169,14 +169,14 @@ def tile_instrumentedlocmblock_pb_t_kernel(
             sums_of[c] = []
             gates_of[c] = []
             for h in range(UNIT_TILES):
-                for unit_tile in (h, UNIT_TILES + h):
-                    units = slice(unit_tile * P, (unit_tile + 1) * P)
+                for i in range(2):
+                    units = slice(i * P, (i + 1) * P)
                     acc = sums_pool.tile([P, 2, CHUNK_ROWS], F32, name="acc", tag="sum")
                     for g in range(PASSES):
                         nc.tensor.matmul_mx(
                             out=acc[:, 0, :],
-                            lhsT=w_codes[:, g, units].bitcast(FP8X4),
-                            lhsT_scale=w_scales[:, g, units],
+                            lhsT=w_codes[h][:, g, units].bitcast(FP8X4),
+                            lhsT_scale=w_scales[h][:, g, units],
                             rhs=y_codes[:, g, :].bitcast(FP8X4),
                             rhs_scale=y_scales[:, g, :],
                             start=(g == 0),
@@ -240,16 +240,17 @@ def tile_instrumentedlocmblock_pb_t_kernel(
             out=bias_bf16[UNIT_TILES : 2 * UNIT_TILES, :], in_=glu_b2.rearrange("(h n) -> h n", n=P)
         )
 
+        warm = const.tile([P, 2], F32)
+        nc.vector.memset(warm[:, 0:1], 0.0)
+        nc.scalar.activation(out=warm[:, 1:2], in_=warm[:, 0:1], func=ACT.Sigmoid)
+
         make_block(0)
         load_added(0, add_groups(0))
         load_last(0)
-        w_rows = const.tile([P, 2 * UNIT_TILES, MODES], BF16)
-        nc.sync.dma_start(
-            out=w_rows[:, 0:UNIT_TILES, :], in_=glu_w1.rearrange("(h q) k -> q h k", q=P)
-        )
-        nc.sync.dma_start(
-            out=w_rows[:, UNIT_TILES : 2 * UNIT_TILES, :], in_=glu_w2.rearrange("(h q) k -> q h k", q=P)
-        )
+        w_rows = const.tile([P, UNIT_TILES, 2, MODES], BF16)
+        for h in range(UNIT_TILES):
+            for i, weights in enumerate((glu_w1, glu_w2)):
+                nc.sync.dma_start(out=w_rows[:, h, i, :], in_=weights[h * P : (h + 1) * P, :])
         load_added(0, add_groups(1))
         for b in range(1, BLOCKS_IN_SBUF):
             load(b)
@@ -272,29 +273,32 @@ def tile_instrumentedlocmblock_pb_t_kernel(
         bias_rows = const.tile([P, P], F32)
         nc.vector.memset(bias_rows[:], 0.0)
         nc.vector.tensor_copy(out=bias_rows[0 : 2 * UNIT_TILES, :], in_=bias_bf16[:])
-        bias_turned = turned_pool.tile([P, PASSES, 2, P], F32, tag="turned")
-        nc.tensor.transpose(bias_turned[:, 0, 0, :], bias_rows[:], ident[:])
+        bias_turned = back_pool.tile([P, CHUNK_GROUPS, UNITS], F32, tag="back")
+        nc.tensor.transpose(bias_turned[:, 0, 0:P], bias_rows[:], ident[:])
         bias_col = const.tile([P, 2 * UNIT_TILES], F32)
-        nc.scalar.copy(out=bias_col[:], in_=bias_turned[:, 0, 0, 0 : 2 * UNIT_TILES])
+        nc.scalar.copy(out=bias_col[:], in_=bias_turned[:, 0, 0 : 2 * UNIT_TILES])
 
         add_chunk(1)
-        w_grouped = const.tile([P, PASSES, 2 * UNITS, 4], BF16, align_bytes=64)
         w_words = w_rows[:].bitcast(F32)
-        for tile_of_units in range(2 * UNIT_TILES):
-            turn(
-                nc,
-                turned_pool,
-                ident,
-                [
-                    [w_words[:, tile_of_units, 2 * g * P + u : 2 * (g + 1) * P : 2] for u in range(2)]
-                    for g in range(PASSES)
-                ],
-                w_grouped[:].bitcast(F32),
-                slice(tile_of_units * P, (tile_of_units + 1) * P),
-            )
-        w_codes = const.tile([P, PASSES, 2 * UNITS], U32, align_bytes=64)
-        w_scales = const.tile([P, PASSES, 2 * UNITS], U8, align_bytes=64)
-        quantise(nc, w_grouped, w_codes, w_scales)
+        w_codes = []
+        w_scales = []
+        for h in range(UNIT_TILES):
+            w_grouped = const.tile([P, PASSES, 2 * P, 4], BF16, name="w_grouped%d" % h, align_bytes=64)
+            for i in range(2):
+                turn(
+                    nc,
+                    turned_pool,
+                    ident,
+                    [
+                        [w_words[:, h, i, 2 * g * P + u : 2 * (g + 1) * P : 2] for u in range(2)]
+                        for g in range(PASSES)
+                    ],
+                    w_grouped[:].bitcast(F32),
+                    slice(i * P, (i + 1) * P),
+                )
+            w_codes.append(const.tile([P, PASSES, 2 * P], U32, name="w_codes%d" % h, align_bytes=64))
+            w_scales.append(const.tile([P, PASSES, 2 * P], U8, name="w_scales%d" % h, align_bytes=64))
+            quantise(nc, w_grouped, w_codes[h], w_scales[h])
 
         for c in range(CHUNKS + 1):
             if c % 2 == 0 and c // 2 + BLOCKS_IN_SBUF < BLOCKS:

@@ -16,18 +16,19 @@ ROWS, MODES, UNITS = 4096, 1024, 256
 K_PASS = 4 * P
 PASSES = MODES // K_PASS
 UNIT_TILES = UNITS // P
+GATE, VALUE = 0, 1
 HALF = P // 2
 
 BLOCK_ROWS = 512
 BLOCKS = ROWS // BLOCK_ROWS
-ADD_GROUPS = 3
-ADD_ROWS = ADD_GROUPS * P
+GROUPS = BLOCK_ROWS // P
+ADD_GROUPS = (2,) + (BLOCKS - 1) * (3,)
 BLOCKS_IN_SBUF = 4
 
 CHUNK_GROUPS = 2
 CHUNK_ROWS = CHUNK_GROUPS * P
 CHUNKS = ROWS // CHUNK_ROWS
-GROUPS_OF_CHUNK = ((ADD_GROUPS, 0), (1, 2))
+GROUPS_OF_CHUNK = {2: ((2, 0), (3, 1)), 3: ((3, 0), (1, 2))}
 
 FLOPS = 2 * ROWS * MODES * 2 * UNITS
 
@@ -76,14 +77,15 @@ def tile_instrumentedlocmblock_pb_t_kernel(
 
     def rows_of(tensor, b):
         rows = tensor[b * BLOCK_ROWS : (b + 1) * BLOCK_ROWS, :]
-        return rows[0:ADD_ROWS, :].rearrange("(q j) k -> q j k", q=P), rows[ADD_ROWS:BLOCK_ROWS, :]
+        add_rows = ADD_GROUPS[b] * P
+        return rows[0:add_rows, :].rearrange("(q j) k -> q j k", q=P), rows[add_rows:BLOCK_ROWS, :]
 
     with ExitStack() as ctx:
         const = ctx.enter_context(tc.tile_pool(name="const", bufs=1))
         loads = ctx.enter_context(tc.tile_pool(name="loads", bufs=BLOCKS_IN_SBUF))
         work = ctx.enter_context(tc.tile_pool(name="work", bufs=2))
-        turned_pool = ctx.enter_context(tc.psum_pool(name="turned", bufs=2))
-        sums_pool = ctx.enter_context(tc.psum_pool(name="sums", bufs=2 * UNIT_TILES))
+        turned_pool = ctx.enter_context(tc.psum_pool(name="turned", bufs=3))
+        sums_pool = ctx.enter_context(tc.psum_pool(name="sums", bufs=3))
         back_pool = ctx.enter_context(tc.psum_pool(name="back", bufs=2))
         ctx.enter_context(tc.manual_schedule())
 
@@ -93,39 +95,50 @@ def tile_instrumentedlocmblock_pb_t_kernel(
         quantised = {}
         sums_of = {}
         gates_of = {}
-        product_of = {}
         result_of = {}
+        product_of = {}
 
-        def add_groups(c):
-            groups = [group for group in GROUPS_OF_CHUNK[c % 2] if group < ADD_GROUPS]
-            return slice(groups[0], groups[-1] + 1)
+        def groups_of(c):
+            count = ADD_GROUPS[c // 2]
+            groups = GROUPS_OF_CHUNK[count][c % 2]
+            added_groups = [group for group in groups if group < count]
+            return (
+                slice(added_groups[0], added_groups[-1] + 1),
+                [group - count for group in groups if group >= count],
+            )
 
         def make_block(b):
+            count = ADD_GROUPS[b]
             loaded[b] = (
-                loads.tile([P, ADD_GROUPS, MODES], BF16, name="y_rows"),
-                loads.tile([P, ADD_GROUPS, MODES], BF16, name="z_rows"),
-                loads.tile([P, 2, MODES], BF16, name="yz_rows"),
+                loads.tile([P, count, MODES], BF16, name="y_rows"),
+                loads.tile([P, count, MODES], BF16, name="z_rows"),
+                [
+                    loads.tile([P, 2, MODES], BF16, name="yz_rows%d" % n)
+                    for n in range(GROUPS - count)
+                ],
             )
 
         def load_added(b, groups):
             for rows, tensor in zip(loaded[b], (y_tilde, z_next)):
                 nc.sync.dma_start(out=rows[:, groups, :], in_=rows_of(tensor, b)[0][:, groups, :])
 
-        def load_last(b):
-            for first, tensor in enumerate((y_tilde, z_next)):
-                nc.sync.dma_start(
-                    out=loaded[b][2][first:P:2, :, :],
-                    in_=rows_of(tensor, b)[1].rearrange("(i q) k -> q i k", q=HALF),
-                )
+        def load_last(b, numbers):
+            for n in numbers:
+                for first, tensor in enumerate((y_tilde, z_next)):
+                    rows = rows_of(tensor, b)[1][n * P : (n + 1) * P, :]
+                    nc.sync.dma_start(
+                        out=loaded[b][2][n][first:P:2, :, :],
+                        in_=rows.rearrange("(i q) k -> q i k", q=HALF),
+                    )
 
         def load(b):
             make_block(b)
-            load_added(b, slice(0, ADD_GROUPS))
-            load_last(b)
+            load_added(b, slice(0, ADD_GROUPS[b]))
+            load_last(b, range(GROUPS - ADD_GROUPS[b]))
 
         def add_chunk(c):
             y_rows, z_rows = loaded[c // 2][:2]
-            groups = add_groups(c)
+            groups = groups_of(c)[0]
             y_next = work.tile([P, CHUNK_GROUPS, 2, MODES // 2], BF16)
             for u in range(2):
                 nc.vector.scalar_tensor_tensor(
@@ -141,21 +154,27 @@ def tile_instrumentedlocmblock_pb_t_kernel(
         def turn_chunk(c):
             grouped = work.tile([P, PASSES, CHUNK_ROWS, 4], BF16, align_bytes=64, bufs=3)
             next_words = added[c][:].rearrange("q j u k -> q (j u k)").bitcast(F32)
-            for i, group in enumerate(GROUPS_OF_CHUNK[c % 2]):
-                columns = slice(i * P, (i + 1) * P)
-                if group == ADD_GROUPS:
-                    add_and_turn(nc, turned_pool, select, loaded[c // 2][2], grouped, columns)
-                else:
-                    j = group - add_groups(c).start
-                    first = [[((2 * j + u) * PASSES + g) * P for u in range(2)] for g in range(PASSES)]
-                    turn(
-                        nc,
-                        turned_pool,
-                        ident,
-                        [[next_words[:, word : word + P] for word in pair] for pair in first],
-                        grouped[:].bitcast(F32),
-                        columns,
-                    )
+            groups, last_groups = groups_of(c)
+            for i, n in enumerate(last_groups):
+                add_and_turn(
+                    nc,
+                    turned_pool,
+                    select,
+                    loaded[c // 2][2][n],
+                    grouped,
+                    slice(i * P, (i + 1) * P),
+                )
+            for j in range(groups.stop - groups.start):
+                first = [[((2 * j + u) * PASSES + g) * P for u in range(2)] for g in range(PASSES)]
+                column = (len(last_groups) + j) * P
+                turn(
+                    nc,
+                    turned_pool,
+                    ident,
+                    [[next_words[:, word : word + P] for word in pair] for pair in first],
+                    grouped[:].bitcast(F32),
+                    slice(column, column + P),
+                )
             grouped_of[c] = grouped
 
         def quantise_chunk(c):
@@ -169,12 +188,12 @@ def tile_instrumentedlocmblock_pb_t_kernel(
             sums_of[c] = []
             gates_of[c] = []
             for h in range(UNIT_TILES):
-                for i in range(2):
+                acc = sums_pool.tile([P, 2, CHUNK_ROWS], F32, tag="sum")
+                for i in (VALUE, GATE):
                     units = slice(i * P, (i + 1) * P)
-                    acc = sums_pool.tile([P, 2, CHUNK_ROWS], F32, name="acc", tag="sum")
                     for g in range(PASSES):
                         nc.tensor.matmul_mx(
-                            out=acc[:, 0, :],
+                            out=acc[:, i, :],
                             lhsT=w_codes[h][:, g, units].bitcast(FP8X4),
                             lhsT_scale=w_scales[h][:, g, units],
                             rhs=y_codes[:, g, :].bitcast(FP8X4),
@@ -182,11 +201,11 @@ def tile_instrumentedlocmblock_pb_t_kernel(
                             start=(g == 0),
                             stop=(g == PASSES - 1),
                         )
-                    sums_of[c].append(acc)
+                sums_of[c].append(acc)
                 gate = work.tile([P, CHUNK_ROWS], F32, bufs=2 * UNIT_TILES)
                 nc.scalar.activation(
                     out=gate[:],
-                    in_=sums_of[c][2 * h][:, 0, :],
+                    in_=acc[:, GATE, :],
                     func=ACT.Sigmoid,
                     bias=bias_col[:, h : h + 1],
                     scale=1.0,
@@ -198,7 +217,7 @@ def tile_instrumentedlocmblock_pb_t_kernel(
             for h in range(UNIT_TILES):
                 nc.vector.scalar_tensor_tensor(
                     out=product[:, h, :],
-                    in0=sums_of[c][2 * h + 1][:, 0, :],
+                    in0=sums_of[c][h][:, VALUE, :],
                     scalar=bias_col[:, UNIT_TILES + h : UNIT_TILES + h + 1],
                     in1=gates_of[c][h][:],
                     op0=ALU.add,
@@ -216,16 +235,29 @@ def tile_instrumentedlocmblock_pb_t_kernel(
                         product_of[c][:, h, i * P : (i + 1) * P],
                         ident[:],
                     )
+            groups, last_groups = groups_of(c)
+            last_count = GROUPS - ADD_GROUPS[b]
             if c % 2 == 0:
-                result_of[b] = work.tile([P, 1 + ADD_GROUPS, UNITS], F32, name="result", bufs=3)
+                result_of[b] = work.tile([P, GROUPS, UNITS], F32, name="result", bufs=3)
             result = result_of[b]
-            first = CHUNK_GROUPS * (c % 2)
-            nc.scalar.copy(out=result[:, first : first + CHUNK_GROUPS, :], in_=back[:])
+            slots = last_groups + [last_count + group for group in range(groups.start, groups.stop)]
             out_added, out_last = rows_of(out, b)
-            if c % 2 == 0:
-                nc.sync.dma_start(out=out_last, in_=result[:, 0, :])
-            else:
-                nc.sync.dma_start(out=out_added, in_=result[:, 1 : 1 + ADD_GROUPS, :])
+            if b == BLOCKS - 1:
+                for i, slot in enumerate(slots):
+                    nc.scalar.copy(out=result[:, slot, :], in_=back[:, i, :])
+                    rows = (
+                        out_last[slot * P : (slot + 1) * P, :]
+                        if slot < last_count
+                        else out_added[:, slot - last_count, :]
+                    )
+                    nc.sync.dma_start(out=rows, in_=result[:, slot, :])
+                return
+            step = slots[1] - slots[0]
+            nc.scalar.copy(out=result[:, slots[0] : slots[1] + 1 : step, :], in_=back[:])
+            for n in last_groups:
+                nc.sync.dma_start(out=out_last[n * P : (n + 1) * P, :], in_=result[:, n, :])
+            if c % 2 == 1:
+                nc.sync.dma_start(out=out_added, in_=result[:, last_count:GROUPS, :])
 
         ident = const.tile([P, P], F32)
         make_identity(nc, ident[:])
@@ -245,13 +277,14 @@ def tile_instrumentedlocmblock_pb_t_kernel(
         nc.scalar.activation(out=warm[:, 1:2], in_=warm[:, 0:1], func=ACT.Sigmoid)
 
         make_block(0)
-        load_added(0, add_groups(0))
-        load_last(0)
+        load_added(0, groups_of(0)[0])
+        load_last(0, groups_of(0)[1])
         w_rows = const.tile([P, UNIT_TILES, 2, MODES], BF16)
         for h in range(UNIT_TILES):
             for i, weights in enumerate((glu_w1, glu_w2)):
                 nc.sync.dma_start(out=w_rows[:, h, i, :], in_=weights[h * P : (h + 1) * P, :])
-        load_added(0, add_groups(1))
+        load_added(0, groups_of(1)[0])
+        load_last(0, groups_of(1)[1])
         for b in range(1, BLOCKS_IN_SBUF):
             load(b)
 

@@ -33,12 +33,12 @@ GROUPS_OF_CHUNK = {2: ((2, 0), (3, 1)), 3: ((3, 0), (1, 2))}
 FLOPS = 2 * ROWS * MODES * 2 * UNITS
 
 
-def turn(nc, turned_pool, ident, words, grouped_words, columns):
+def turn(nc, turned_pool, ident, words, grouped_words, columns, copy):
     turned = turned_pool.tile([P, PASSES, 2, P], F32, tag="turned")
     for g in range(PASSES):
         for u in range(2):
             nc.tensor.transpose(turned[:, g, u, :], words[g][u], ident[:])
-    nc.scalar.copy(
+    copy(
         out=grouped_words[:, :, columns, :],
         in_=turned[:].rearrange("p g u q -> p g q u"),
     )
@@ -128,7 +128,7 @@ def tile_instrumentedlocmblock_pb_t_kernel(
                     rows = rows_of(tensor, b)[1][n * P : (n + 1) * P, :]
                     nc.sync.dma_start(
                         out=loaded[b][2][n][first:P:2, :, :],
-                        in_=rows.rearrange("(i q) k -> q i k", q=HALF),
+                        in_=rows.rearrange("(q i) k -> q i k", i=2),
                     )
 
         def load(b):
@@ -174,6 +174,7 @@ def tile_instrumentedlocmblock_pb_t_kernel(
                     [[next_words[:, word : word + P] for word in pair] for pair in first],
                     grouped[:].bitcast(F32),
                     slice(column, column + P),
+                    nc.vector.tensor_copy if c == CHUNKS - 1 and j == 1 else nc.scalar.copy,
                 )
             grouped_of[c] = grouped
 
@@ -225,13 +226,25 @@ def tile_instrumentedlocmblock_pb_t_kernel(
                 )
             product_of[c] = product
 
+        def store_last(b, n):
+            rows = rows_of(out, b)[1][n * P : (n + 1) * P, :].rearrange("(q i) n -> i q n", i=2)
+            for i in range(2):
+                nc.sync.dma_start(out=rows[i], in_=result_of[b][i * HALF : (i + 1) * HALF, n, :])
+
         def turn_back_and_store(c):
             b = c // 2
-            back = back_pool.tile([P, CHUNK_GROUPS, UNITS], F32, tag="back")
+            if c == CHUNKS - 1:
+                backs = [
+                    back_pool.tile([P, 2, UNITS], F32, name="back%d" % i, tag="back")[:, 0, :]
+                    for i in range(CHUNK_GROUPS)
+                ]
+            else:
+                back = back_pool.tile([P, CHUNK_GROUPS, UNITS], F32, tag="back")
+                backs = [back[:, i, :] for i in range(CHUNK_GROUPS)]
             for i in range(CHUNK_GROUPS):
                 for h in range(UNIT_TILES):
                     nc.tensor.transpose(
-                        back[:, i, h * P : (h + 1) * P],
+                        backs[i][:, h * P : (h + 1) * P],
                         product_of[c][:, h, i * P : (i + 1) * P],
                         ident[:],
                     )
@@ -241,21 +254,20 @@ def tile_instrumentedlocmblock_pb_t_kernel(
                 result_of[b] = work.tile([P, GROUPS, UNITS], F32, name="result", bufs=3)
             result = result_of[b]
             slots = last_groups + [last_count + group for group in range(groups.start, groups.stop)]
-            out_added, out_last = rows_of(out, b)
+            out_added = rows_of(out, b)[0]
             if b == BLOCKS - 1:
                 for i, slot in enumerate(slots):
-                    nc.scalar.copy(out=result[:, slot, :], in_=back[:, i, :])
-                    rows = (
-                        out_last[slot * P : (slot + 1) * P, :]
-                        if slot < last_count
-                        else out_added[:, slot - last_count, :]
-                    )
-                    nc.sync.dma_start(out=rows, in_=result[:, slot, :])
+                    copy = nc.vector.tensor_copy if c == CHUNKS - 1 and i == 1 else nc.scalar.copy
+                    copy(out=result[:, slot, :], in_=backs[i])
+                    if slot < last_count:
+                        store_last(b, slot)
+                    else:
+                        nc.sync.dma_start(out=out_added[:, slot - last_count, :], in_=result[:, slot, :])
                 return
             step = slots[1] - slots[0]
             nc.scalar.copy(out=result[:, slots[0] : slots[1] + 1 : step, :], in_=back[:])
             for n in last_groups:
-                nc.sync.dma_start(out=out_last[n * P : (n + 1) * P, :], in_=result[:, n, :])
+                store_last(b, n)
             if c % 2 == 1:
                 nc.sync.dma_start(out=out_added, in_=result[:, last_count:GROUPS, :])
 
@@ -328,6 +340,7 @@ def tile_instrumentedlocmblock_pb_t_kernel(
                     ],
                     w_grouped[:].bitcast(F32),
                     slice(i * P, (i + 1) * P),
+                    nc.scalar.copy,
                 )
             w_codes.append(const.tile([P, PASSES, 2 * P], U32, name="w_codes%d" % h, align_bytes=64))
             w_scales.append(const.tile([P, PASSES, 2 * P], U8, name="w_scales%d" % h, align_bytes=64))

@@ -83,7 +83,7 @@ def tile_instrumentedlocmblock_pb_t_kernel(
     with ExitStack() as ctx:
         const = ctx.enter_context(tc.tile_pool(name="const", bufs=1))
         loads = ctx.enter_context(tc.tile_pool(name="loads", bufs=BLOCKS_IN_SBUF))
-        work = ctx.enter_context(tc.tile_pool(name="work", bufs=2))
+        work = ctx.enter_context(tc.tile_pool(name="work", bufs=4))
         turned_pool = ctx.enter_context(tc.psum_pool(name="turned", bufs=3))
         sums_pool = ctx.enter_context(tc.psum_pool(name="sums", bufs=3))
         back_pool = ctx.enter_context(tc.psum_pool(name="back", bufs=2))
@@ -144,7 +144,7 @@ def tile_instrumentedlocmblock_pb_t_kernel(
                 nc.vector.scalar_tensor_tensor(
                     out=y_next[:, 0 : groups.stop - groups.start, u, :].rearrange("q j (w e) -> q j w e", e=2),
                     in0=z_rows[:, groups, :].rearrange("q j (w u e) -> q u j w e", u=2, e=2)[:, u],
-                    scalar=dt_col[:, 0:1],
+                    scalar=consts["dt"][:, 0:1],
                     in1=y_rows[:, groups, :].rearrange("q j (w u e) -> q u j w e", u=2, e=2)[:, u],
                     op0=ALU.mult,
                     op1=ALU.add,
@@ -152,14 +152,14 @@ def tile_instrumentedlocmblock_pb_t_kernel(
             added[c] = y_next
 
         def turn_chunk(c):
-            grouped = work.tile([P, PASSES, CHUNK_ROWS, 4], BF16, align_bytes=64, bufs=3)
+            grouped = work.tile([P, PASSES, CHUNK_ROWS, 4], BF16, align_bytes=64, bufs=5)
             next_words = added[c][:].rearrange("q j u k -> q (j u k)").bitcast(F32)
             groups, last_groups = groups_of(c)
             for i, n in enumerate(last_groups):
                 add_and_turn(
                     nc,
                     turned_pool,
-                    select,
+                    consts["select"],
                     loaded[c // 2][2][n],
                     grouped,
                     slice(i * P, (i + 1) * P),
@@ -203,12 +203,12 @@ def tile_instrumentedlocmblock_pb_t_kernel(
                             stop=(g == PASSES - 1),
                         )
                 sums_of[c].append(acc)
-                gate = work.tile([P, CHUNK_ROWS], F32, bufs=2 * UNIT_TILES)
+                gate = work.tile([P, CHUNK_ROWS], F32, bufs=4 * UNIT_TILES)
                 nc.scalar.activation(
                     out=gate[:],
                     in_=acc[:, GATE, :],
                     func=ACT.Sigmoid,
-                    bias=bias_col[:, h : h + 1],
+                    bias=consts["bias"][:, h : h + 1],
                     scale=1.0,
                 )
                 gates_of[c].append(gate)
@@ -219,7 +219,7 @@ def tile_instrumentedlocmblock_pb_t_kernel(
                 nc.vector.scalar_tensor_tensor(
                     out=product[:, h, :],
                     in0=sums_of[c][h][:, VALUE, :],
-                    scalar=bias_col[:, UNIT_TILES + h : UNIT_TILES + h + 1],
+                    scalar=consts["bias"][:, UNIT_TILES + h : UNIT_TILES + h + 1],
                     in1=gates_of[c][h][:],
                     op0=ALU.add,
                     op1=ALU.mult,
@@ -251,7 +251,7 @@ def tile_instrumentedlocmblock_pb_t_kernel(
             groups, last_groups = groups_of(c)
             last_count = GROUPS - ADD_GROUPS[b]
             if c % 2 == 0:
-                result_of[b] = work.tile([P, GROUPS, UNITS], F32, name="result", bufs=3)
+                result_of[b] = work.tile([P, GROUPS, UNITS], F32, name="result", bufs=BLOCKS)
             result = result_of[b]
             slots = last_groups + [last_count + group for group in range(groups.start, groups.stop)]
             out_added = rows_of(out, b)[0]
@@ -288,47 +288,19 @@ def tile_instrumentedlocmblock_pb_t_kernel(
         nc.vector.memset(warm[:, 0:1], 0.0)
         nc.scalar.activation(out=warm[:, 1:2], in_=warm[:, 0:1], func=ACT.Sigmoid)
 
-        make_block(0)
-        load_added(0, groups_of(0)[0])
-        load_last(0, groups_of(0)[1])
         w_rows = const.tile([P, UNIT_TILES, 2, MODES], BF16)
-        for h in range(UNIT_TILES):
-            for i, weights in enumerate((glu_w1, glu_w2)):
-                nc.sync.dma_start(out=w_rows[:, h, i, :], in_=weights[h * P : (h + 1) * P, :])
-        load_added(0, groups_of(1)[0])
-        load_last(0, groups_of(1)[1])
-        for b in range(1, BLOCKS_IN_SBUF):
-            load(b)
-
-        dt_col = const.tile([P, 1], F32)
-        nc.vector.tensor_copy(out=dt_col[:], in_=dt_bf16[:])
-        select = const.tile([P, HALF], BF16)
-        nc.vector.scalar_tensor_tensor(
-            out=select[:],
-            in0=ident[:, 1:P:2],
-            scalar=dt_col[:, 0:1],
-            in1=ident[:, 0:P:2],
-            op0=ALU.mult,
-            op1=ALU.add,
-        )
-
-        add_chunk(0)
-        turn_chunk(0)
-
-        bias_rows = const.tile([P, P], F32)
-        nc.vector.memset(bias_rows[:], 0.0)
-        nc.vector.tensor_copy(out=bias_rows[0 : 2 * UNIT_TILES, :], in_=bias_bf16[:])
-        bias_turned = back_pool.tile([P, CHUNK_GROUPS, UNITS], F32, tag="back")
-        nc.tensor.transpose(bias_turned[:, 0, 0:P], bias_rows[:], ident[:])
-        bias_col = const.tile([P, 2 * UNIT_TILES], F32)
-        nc.scalar.copy(out=bias_col[:], in_=bias_turned[:, 0, 0 : 2 * UNIT_TILES])
-
-        add_chunk(1)
         w_words = w_rows[:].bitcast(F32)
         w_codes = []
         w_scales = []
-        for h in range(UNIT_TILES):
-            w_grouped = const.tile([P, PASSES, 2 * P, 4], BF16, name="w_grouped%d" % h, align_bytes=64)
+        w_grouped = []
+        consts = {}
+
+        def load_weights(h):
+            for i, weights in enumerate((glu_w1, glu_w2)):
+                nc.sync.dma_start(out=w_rows[:, h, i, :], in_=weights[h * P : (h + 1) * P, :])
+
+        def turn_weights(h):
+            w_grouped.append(const.tile([P, PASSES, 2 * P, 4], BF16, name="w_grouped%d" % h, align_bytes=64))
             for i in range(2):
                 turn(
                     nc,
@@ -338,13 +310,68 @@ def tile_instrumentedlocmblock_pb_t_kernel(
                         [w_words[:, h, i, 2 * g * P + u : 2 * (g + 1) * P : 2] for u in range(2)]
                         for g in range(PASSES)
                     ],
-                    w_grouped[:].bitcast(F32),
+                    w_grouped[h][:].bitcast(F32),
                     slice(i * P, (i + 1) * P),
                     nc.scalar.copy,
                 )
+
+        def quantise_weights(h):
             w_codes.append(const.tile([P, PASSES, 2 * P], U32, name="w_codes%d" % h, align_bytes=64))
             w_scales.append(const.tile([P, PASSES, 2 * P], U8, name="w_scales%d" % h, align_bytes=64))
-            quantise(nc, w_grouped, w_codes[h], w_scales[h])
+            quantise(nc, w_grouped[h], w_codes[h], w_scales[h])
+
+        def make_dt():
+            dt_col = const.tile([P, 1], F32, name="dt_col")
+            nc.vector.tensor_copy(out=dt_col[:], in_=dt_bf16[:])
+            select = const.tile([P, HALF], BF16, name="select")
+            nc.vector.scalar_tensor_tensor(
+                out=select[:],
+                in0=ident[:, 1:P:2],
+                scalar=dt_col[:, 0:1],
+                in1=ident[:, 0:P:2],
+                op0=ALU.mult,
+                op1=ALU.add,
+            )
+            consts["dt"] = dt_col
+            consts["select"] = select
+
+        def lay_biases():
+            bias_rows = const.tile([P, P], F32, name="bias_rows")
+            nc.vector.memset(bias_rows[:], 0.0)
+            nc.vector.tensor_copy(out=bias_rows[0 : 2 * UNIT_TILES, :], in_=bias_bf16[:])
+            consts["bias_rows"] = bias_rows
+
+        def turn_biases():
+            bias_turned = back_pool.tile([P, CHUNK_GROUPS, UNITS], F32, tag="back")
+            nc.tensor.transpose(bias_turned[:, 0, 0:P], consts["bias_rows"][:], ident[:])
+            bias_col = const.tile([P, 2 * UNIT_TILES], F32, name="bias_col")
+            nc.scalar.copy(out=bias_col[:], in_=bias_turned[:, 0, 0 : 2 * UNIT_TILES])
+            consts["bias"] = bias_col
+
+        make_block(0)
+        load_added(0, groups_of(0)[0])
+        load_last(0, groups_of(0)[1])
+        load_weights(0)
+        load_weights(1)
+        load_added(0, groups_of(1)[0])
+        load_last(0, groups_of(1)[1])
+        make_block(1)
+        load_added(1, groups_of(2)[0])
+        load_last(1, groups_of(2)[1])
+        load_added(1, groups_of(3)[0])
+        for b in range(2, BLOCKS_IN_SBUF):
+            load(b)
+
+        make_dt()
+        lay_biases()
+        add_chunk(0)
+        turn_chunk(0)
+        turn_weights(0)
+        add_chunk(1)
+        quantise_weights(0)
+        turn_weights(1)
+        quantise_weights(1)
+        turn_biases()
 
         for c in range(CHUNKS + 1):
             if c % 2 == 0 and c // 2 + BLOCKS_IN_SBUF < BLOCKS:

@@ -23,7 +23,7 @@ BLOCK_ROWS = 512
 BLOCKS = ROWS // BLOCK_ROWS
 GROUPS = BLOCK_ROWS // P
 ADD_GROUPS = (2,) + (BLOCKS - 1) * (3,)
-BLOCKS_IN_SBUF = 4
+BLOCKS_IN_SBUF = 6
 
 CHUNK_GROUPS = 2
 CHUNK_ROWS = CHUNK_GROUPS * P
@@ -113,7 +113,7 @@ def tile_instrumentedlocmblock_pb_t_kernel(
                 loads.tile([P, count, MODES], BF16, name="y_rows"),
                 loads.tile([P, count, MODES], BF16, name="z_rows"),
                 [
-                    loads.tile([P, 2, MODES], BF16, name="yz_rows%d" % n)
+                    loads.tile([P, 2, MODES], BF16, name="yz_rows%d" % n, bufs=1 if n else BLOCKS_IN_SBUF)
                     for n in range(GROUPS - count)
                 ],
             )
@@ -323,6 +323,10 @@ def tile_instrumentedlocmblock_pb_t_kernel(
         def make_dt():
             dt_col = const.tile([P, 1], F32, name="dt_col")
             nc.vector.tensor_copy(out=dt_col[:], in_=dt_bf16[:])
+            consts["dt"] = dt_col
+
+        def make_select():
+            dt_col = consts["dt"]
             select = const.tile([P, HALF], BF16, name="select")
             nc.vector.scalar_tensor_tensor(
                 out=select[:],
@@ -332,7 +336,6 @@ def tile_instrumentedlocmblock_pb_t_kernel(
                 op0=ALU.mult,
                 op1=ALU.add,
             )
-            consts["dt"] = dt_col
             consts["select"] = select
 
         def lay_biases():
@@ -363,8 +366,9 @@ def tile_instrumentedlocmblock_pb_t_kernel(
             load(b)
 
         make_dt()
-        lay_biases()
         add_chunk(0)
+        make_select()
+        lay_biases()
         turn_chunk(0)
         turn_weights(0)
         add_chunk(1)

@@ -23,7 +23,6 @@ BLOCK_ROWS = 512
 BLOCKS = ROWS // BLOCK_ROWS
 GROUPS = BLOCK_ROWS // P
 ADD_GROUPS = (2,) + (BLOCKS - 1) * (3,)
-BLOCKS_IN_SBUF = 6
 
 CHUNK_GROUPS = 2
 CHUNK_ROWS = CHUNK_GROUPS * P
@@ -82,8 +81,8 @@ def tile_instrumentedlocmblock_pb_t_kernel(
 
     with ExitStack() as ctx:
         const = ctx.enter_context(tc.tile_pool(name="const", bufs=1))
-        loads = ctx.enter_context(tc.tile_pool(name="loads", bufs=BLOCKS_IN_SBUF))
-        work = ctx.enter_context(tc.tile_pool(name="work", bufs=4))
+        loads = ctx.enter_context(tc.tile_pool(name="loads", bufs=BLOCKS))
+        work = ctx.enter_context(tc.tile_pool(name="work", bufs=3))
         turned_pool = ctx.enter_context(tc.psum_pool(name="turned", bufs=3))
         sums_pool = ctx.enter_context(tc.psum_pool(name="sums", bufs=3))
         back_pool = ctx.enter_context(tc.psum_pool(name="back", bufs=2))
@@ -113,7 +112,7 @@ def tile_instrumentedlocmblock_pb_t_kernel(
                 loads.tile([P, count, MODES], BF16, name="y_rows"),
                 loads.tile([P, count, MODES], BF16, name="z_rows"),
                 [
-                    loads.tile([P, 2, MODES], BF16, name="yz_rows%d" % n, bufs=1 if n else BLOCKS_IN_SBUF)
+                    loads.tile([P, 2, MODES], BF16, name="yz_rows%d" % n, bufs=1 if n else BLOCKS)
                     for n in range(GROUPS - count)
                 ],
             )
@@ -144,7 +143,7 @@ def tile_instrumentedlocmblock_pb_t_kernel(
                 nc.vector.scalar_tensor_tensor(
                     out=y_next[:, 0 : groups.stop - groups.start, u, :].rearrange("q j (w e) -> q j w e", e=2),
                     in0=z_rows[:, groups, :].rearrange("q j (w u e) -> q u j w e", u=2, e=2)[:, u],
-                    scalar=consts["dt"][:, 0:1],
+                    scalar=dt_bf16[:, 0:1],
                     in1=y_rows[:, groups, :].rearrange("q j (w u e) -> q u j w e", u=2, e=2)[:, u],
                     op0=ALU.mult,
                     op1=ALU.add,
@@ -152,7 +151,7 @@ def tile_instrumentedlocmblock_pb_t_kernel(
             added[c] = y_next
 
         def turn_chunk(c):
-            grouped = work.tile([P, PASSES, CHUNK_ROWS, 4], BF16, align_bytes=64, bufs=5)
+            grouped = work.tile([P, PASSES, CHUNK_ROWS, 4], BF16, align_bytes=64, bufs=4)
             next_words = added[c][:].rearrange("q j u k -> q (j u k)").bitcast(F32)
             groups, last_groups = groups_of(c)
             for i, n in enumerate(last_groups):
@@ -203,7 +202,7 @@ def tile_instrumentedlocmblock_pb_t_kernel(
                             stop=(g == PASSES - 1),
                         )
                 sums_of[c].append(acc)
-                gate = work.tile([P, CHUNK_ROWS], F32, bufs=4 * UNIT_TILES)
+                gate = work.tile([P, CHUNK_ROWS], F32, bufs=3 * UNIT_TILES)
                 nc.scalar.activation(
                     out=gate[:],
                     in_=acc[:, GATE, :],
@@ -320,22 +319,18 @@ def tile_instrumentedlocmblock_pb_t_kernel(
             w_scales.append(const.tile([P, PASSES, 2 * P], U8, name="w_scales%d" % h, align_bytes=64))
             quantise(nc, w_grouped[h], w_codes[h], w_scales[h])
 
-        def make_dt():
-            dt_col = const.tile([P, 1], F32, name="dt_col")
-            nc.vector.tensor_copy(out=dt_col[:], in_=dt_bf16[:])
-            consts["dt"] = dt_col
-
         def make_select():
-            dt_col = consts["dt"]
-            select = const.tile([P, HALF], BF16, name="select")
-            nc.vector.scalar_tensor_tensor(
-                out=select[:],
+            dt_part = const.tile([P, HALF], F32, name="dt_part")
+            nc.gpsimd.tensor_scalar(
+                out=dt_part[:],
                 in0=ident[:, 1:P:2],
-                scalar=dt_col[:, 0:1],
-                in1=ident[:, 0:P:2],
+                scalar1=dt_bf16[:, 0:1],
+                scalar2=0.0,
                 op0=ALU.mult,
                 op1=ALU.add,
             )
+            select = const.tile([P, HALF], BF16, name="select")
+            nc.gpsimd.tensor_tensor(out=select[:], in0=dt_part[:], in1=ident[:, 0:P:2], op=ALU.add)
             consts["select"] = select
 
         def lay_biases():
@@ -362,12 +357,11 @@ def tile_instrumentedlocmblock_pb_t_kernel(
         load_added(1, groups_of(2)[0])
         load_last(1, groups_of(2)[1])
         load_added(1, groups_of(3)[0])
-        for b in range(2, BLOCKS_IN_SBUF):
+        for b in range(2, BLOCKS):
             load(b)
 
-        make_dt()
-        add_chunk(0)
         make_select()
+        add_chunk(0)
         lay_biases()
         turn_chunk(0)
         turn_weights(0)
@@ -378,8 +372,6 @@ def tile_instrumentedlocmblock_pb_t_kernel(
         turn_biases()
 
         for c in range(CHUNKS + 1):
-            if c % 2 == 0 and c // 2 + BLOCKS_IN_SBUF < BLOCKS:
-                load(c // 2 + BLOCKS_IN_SBUF)
             if c < CHUNKS:
                 quantise_chunk(c)
             if c >= 1:

@@ -212,6 +212,50 @@ def tile_instrumentedlocmblock_pb_t_kernel(
                 )
                 gates_of[c].append(gate)
 
+        def multiply_group(c, r):
+            y_codes, y_scales = quantised[c]
+            rows = slice(r * P, (r + 1) * P)
+            product = work.tile([P, UNIT_TILES, P], F32, name="last_product")
+            for h in range(UNIT_TILES):
+                pool, tag = (sums_pool, "sum") if (r, h) == (1, 1) else (turned_pool, "turned")
+                acc = pool.tile([P, 2, 2, P], F32, name="last_sums", tag=tag)
+                for i in (VALUE, GATE):
+                    units = slice(i * P, (i + 1) * P)
+                    for g in range(PASSES):
+                        nc.tensor.matmul_mx(
+                            out=acc[:, 0, i, :],
+                            lhsT=w_codes[h][:, g, units].bitcast(FP8X4),
+                            lhsT_scale=w_scales[h][:, g, units],
+                            rhs=y_codes[:, g, rows].bitcast(FP8X4),
+                            rhs_scale=y_scales[:, g, rows],
+                            start=(g == 0),
+                            stop=(g == PASSES - 1),
+                        )
+                gate = work.tile([P, P], F32, name="last_gate")
+                nc.scalar.activation(out=gate[:], in_=acc[:, 0, GATE, :], func=ACT.Sigmoid, bias=consts["bias"][:, h : h + 1], scale=1.0)
+                nc.vector.scalar_tensor_tensor(
+                    out=product[:, h, :],
+                    in0=acc[:, 0, VALUE, :],
+                    scalar=consts["bias"][:, UNIT_TILES + h : UNIT_TILES + h + 1],
+                    in1=gate[:],
+                    op0=ALU.add,
+                    op1=ALU.mult,
+                )
+            last_products.append(product)
+
+        def back_group(c, r):
+            b = c // 2
+            slot = 1 + groups_of(c)[0].start + r
+            pool, tag = ((back_pool, "back"), (sums_pool, "sum"))[r]
+            back = pool.tile([P, CHUNK_GROUPS, UNITS], F32, name="last_back", tag=tag)
+            for h in range(UNIT_TILES):
+                nc.tensor.transpose(back[:, 0, h * P : (h + 1) * P], last_products[r][:, h, :], ident[:])
+            copy = (nc.scalar.copy, nc.vector.tensor_copy)[r]
+            copy(out=result_of[b][:, slot, :], in_=back[:, 0, :])
+            nc.sync.dma_start(out=rows_of(out, b)[0][:, slot - 1, :], in_=result_of[b][:, slot, :])
+
+        last_products = []
+
         def gate_chunk(c):
             product = work.tile([P, UNIT_TILES, CHUNK_ROWS], F32)
             for h in range(UNIT_TILES):
@@ -371,16 +415,21 @@ def tile_instrumentedlocmblock_pb_t_kernel(
         quantise_weights(1)
         turn_biases()
 
-        for c in range(CHUNKS + 1):
-            if c < CHUNKS:
-                quantise_chunk(c)
+        for c in range(CHUNKS - 1):
+            quantise_chunk(c)
             if c >= 1:
                 gate_chunk(c - 1)
             if c + 2 < CHUNKS:
                 add_chunk(c + 2)
-            if c + 1 < CHUNKS:
-                turn_chunk(c + 1)
-            if c < CHUNKS:
-                multiply_chunk(c)
+            turn_chunk(c + 1)
+            multiply_chunk(c)
             if c >= 1:
                 turn_back_and_store(c - 1)
+        c = CHUNKS - 1
+        quantise_chunk(c)
+        gate_chunk(c - 1)
+        multiply_group(c, 0)
+        multiply_group(c, 1)
+        turn_back_and_store(c - 1)
+        back_group(c, 0)
+        back_group(c, 1)

from contextlib import ExitStack

import concourse.mybir as mybir
from concourse.masks import make_identity

BF16 = mybir.dt.bfloat16
F32 = mybir.dt.float32
U32 = mybir.dt.uint32
U8 = mybir.dt.uint8
FP8X4 = mybir.dt.float8_e4m3fn_x4
ACT = mybir.ActivationFunctionType
ALU = mybir.AluOpType

P = 128
ROWS, MODES, UNITS = 4096, 1024, 256
K_PASS = 4 * P
PASSES = MODES // K_PASS
UNIT_TILES = UNITS // P
GATE, VALUE = 0, 1
HALF = P // 2

BLOCK_ROWS = 512
BLOCKS = ROWS // BLOCK_ROWS
GROUPS = BLOCK_ROWS // P
ADD_GROUPS = (2,) + (BLOCKS - 1) * (3,)

CHUNK_GROUPS = 2
CHUNK_ROWS = CHUNK_GROUPS * P
CHUNKS = ROWS // CHUNK_ROWS
GROUPS_OF_CHUNK = {2: ((2, 0), (3, 1)), 3: ((3, 0), (1, 2))}

FLOPS = 2 * ROWS * MODES * 2 * UNITS


def turn(nc, turned_pool, ident, words, grouped_words, columns, copy):
    turned = turned_pool.tile([P, PASSES, 2, P], F32, tag="turned")
    for g in range(PASSES):
        for u in range(2):
            nc.tensor.transpose(turned[:, g, u, :], words[g][u], ident[:])
    copy(
        out=grouped_words[:, :, columns, :],
        in_=turned[:].rearrange("p g u q -> p g q u"),
    )


def add_and_turn(nc, turned_pool, select, yz_rows, grouped, columns):
    turned = turned_pool.tile([P, PASSES, 4, P], BF16, tag="turned")
    for i in range(2):
        for g in range(PASSES):
            for t in range(4):
                nc.tensor.matmul(
                    out=turned[:, g, t, i * HALF : (i + 1) * HALF],
                    lhsT=yz_rows[:, i, g * K_PASS + t : (g + 1) * K_PASS : 4],
                    rhs=select[:],
                    start=True,
                    stop=True,
                )
    nc.scalar.copy(
        out=grouped[:, :, columns, :],
        in_=turned[:].rearrange("p g t q -> p g q t"),
    )


def quantise(nc, grouped, codes, scales):
    nc.vector.quantize_mx(
        out=codes[:].rearrange("p g c -> p (g c)").bitcast(FP8X4),
        scales=scales[:].rearrange("p g c -> p (g c)"),
        in_=grouped[:].rearrange("p g c t -> p (g c t)"),
    )


def tile_instrumentedlocmblock_pb_t_kernel(
    tc, y_tilde, z_next, dt, glu_w1, glu_w2, glu_b1, glu_b2, out
):
    nc = tc.nc

    def rows_of(tensor, b):
        rows = tensor[b * BLOCK_ROWS : (b + 1) * BLOCK_ROWS, :]
        add_rows = ADD_GROUPS[b] * P
        return rows[0:add_rows, :].rearrange("(q j) k -> q j k", q=P), rows[add_rows:BLOCK_ROWS, :]

    with ExitStack() as ctx:
        const = ctx.enter_context(tc.tile_pool(name="const", bufs=1))
        loads = ctx.enter_context(tc.tile_pool(name="loads", bufs=BLOCKS))
        work = ctx.enter_context(tc.tile_pool(name="work", bufs=3))
        turned_pool = ctx.enter_context(tc.psum_pool(name="turned", bufs=3))
        sums_pool = ctx.enter_context(tc.psum_pool(name="sums", bufs=3))
        back_pool = ctx.enter_context(tc.psum_pool(name="back", bufs=2))
        ctx.enter_context(tc.manual_schedule())

        loaded = {}
        added = {}
        grouped_of = {}
        quantised = {}
        sums_of = {}
        gates_of = {}
        result_of = {}
        product_of = {}

        def groups_of(c):
            count = ADD_GROUPS[c // 2]
            groups = GROUPS_OF_CHUNK[count][c % 2]
            added_groups = [group for group in groups if group < count]
            return (
                slice(added_groups[0], added_groups[-1] + 1),
                [group - count for group in groups if group >= count],
            )

        def make_block(b):
            count = ADD_GROUPS[b]
            loaded[b] = (
                loads.tile([P, count, MODES], BF16, name="y_rows"),
                loads.tile([P, count, MODES], BF16, name="z_rows"),
                [
                    loads.tile([P, 2, MODES], BF16, name="yz_rows%d" % n, bufs=1 if n else BLOCKS)
                    for n in range(GROUPS - count)
                ],
            )

        def load_added(b, groups):
            for rows, tensor in zip(loaded[b], (y_tilde, z_next)):
                nc.sync.dma_start(out=rows[:, groups, :], in_=rows_of(tensor, b)[0][:, groups, :])

        def load_last(b, numbers):
            for n in numbers:
                for first, tensor in enumerate((y_tilde, z_next)):
                    rows = rows_of(tensor, b)[1][n * P : (n + 1) * P, :]
                    nc.sync.dma_start(
                        out=loaded[b][2][n][first:P:2, :, :],
                        in_=rows.rearrange("(q i) k -> q i k", i=2),
                    )

        def load(b):
            make_block(b)
            load_added(b, slice(0, ADD_GROUPS[b]))
            load_last(b, range(GROUPS - ADD_GROUPS[b]))

        def add_chunk(c):
            y_rows, z_rows = loaded[c // 2][:2]
            groups = groups_of(c)[0]
            y_next = work.tile([P, CHUNK_GROUPS, 2, MODES // 2], BF16)
            for u in range(2):
                nc.vector.scalar_tensor_tensor(
                    out=y_next[:, 0 : groups.stop - groups.start, u, :].rearrange("q j (w e) -> q j w e", e=2),
                    in0=z_rows[:, groups, :].rearrange("q j (w u e) -> q u j w e", u=2, e=2)[:, u],
                    scalar=dt_bf16[:, 0:1],
                    in1=y_rows[:, groups, :].rearrange("q j (w u e) -> q u j w e", u=2, e=2)[:, u],
                    op0=ALU.mult,
                    op1=ALU.add,
                )
            added[c] = y_next

        def turn_chunk(c):
            grouped = work.tile([P, PASSES, CHUNK_ROWS, 4], BF16, align_bytes=64, bufs=4)
            next_words = added[c][:].rearrange("q j u k -> q (j u k)").bitcast(F32)
            groups, last_groups = groups_of(c)
            for i, n in enumerate(last_groups):
                add_and_turn(
                    nc,
                    turned_pool,
                    consts["select"],
                    loaded[c // 2][2][n],
                    grouped,
                    slice(i * P, (i + 1) * P),
                )
            for j in range(groups.stop - groups.start):
                first = [[((2 * j + u) * PASSES + g) * P for u in range(2)] for g in range(PASSES)]
                column = (len(last_groups) + j) * P
                turn(
                    nc,
                    turned_pool,
                    ident,
                    [[next_words[:, word : word + P] for word in pair] for pair in first],
                    grouped[:].bitcast(F32),
                    slice(column, column + P),
                    nc.vector.tensor_copy if c == CHUNKS - 1 and j == 1 else nc.scalar.copy,
                )
            grouped_of[c] = grouped

        def quantise_chunk(c):
            y_codes = work.tile([P, PASSES, CHUNK_ROWS], U32, align_bytes=64)
            y_scales = work.tile([P, PASSES, CHUNK_ROWS], U8, align_bytes=64)
            quantise(nc, grouped_of[c], y_codes, y_scales)
            quantised[c] = (y_codes, y_scales)

        def multiply_chunk(c):
            y_codes, y_scales = quantised[c]
            sums_of[c] = []
            gates_of[c] = []
            for h in range(UNIT_TILES):
                acc = sums_pool.tile([P, 2, CHUNK_ROWS], F32, tag="sum")
                for i in (VALUE, GATE):
                    units = slice(i * P, (i + 1) * P)
                    for g in range(PASSES):
                        nc.tensor.matmul_mx(
                            out=acc[:, i, :],
                            lhsT=w_codes[h][:, g, units].bitcast(FP8X4),
                            lhsT_scale=w_scales[h][:, g, units],
                            rhs=y_codes[:, g, :].bitcast(FP8X4),
                            rhs_scale=y_scales[:, g, :],
                            start=(g == 0),
                            stop=(g == PASSES - 1),
                        )
                sums_of[c].append(acc)
                gate = work.tile([P, CHUNK_ROWS], F32, bufs=3 * UNIT_TILES)
                nc.scalar.activation(
                    out=gate[:],
                    in_=acc[:, GATE, :],
                    func=ACT.Sigmoid,
                    bias=consts["bias"][:, h : h + 1],
                    scale=1.0,
                )
                gates_of[c].append(gate)

        def multiply_group(c, r):
            y_codes, y_scales = quantised[c]
            rows = slice(r * P, (r + 1) * P)
            product = work.tile([P, UNIT_TILES, P], F32, name="last_product")
            for h in range(UNIT_TILES):
                pool, tag = (sums_pool, "sum") if (r, h) == (1, 1) else (turned_pool, "turned")
                acc = pool.tile([P, 2, 2, P], F32, name="last_sums", tag=tag)
                for i in (VALUE, GATE):
                    units = slice(i * P, (i + 1) * P)
                    for g in range(PASSES):
                        nc.tensor.matmul_mx(
                            out=acc[:, 0, i, :],
                            lhsT=w_codes[h][:, g, units].bitcast(FP8X4),
                            lhsT_scale=w_scales[h][:, g, units],
                            rhs=y_codes[:, g, rows].bitcast(FP8X4),
                            rhs_scale=y_scales[:, g, rows],
                            start=(g == 0),
                            stop=(g == PASSES - 1),
                        )
                gate = work.tile([P, P], F32, name="last_gate")
                nc.scalar.activation(out=gate[:], in_=acc[:, 0, GATE, :], func=ACT.Sigmoid, bias=consts["bias"][:, h : h + 1], scale=1.0)
                nc.vector.scalar_tensor_tensor(
                    out=product[:, h, :],
                    in0=acc[:, 0, VALUE, :],
                    scalar=consts["bias"][:, UNIT_TILES + h : UNIT_TILES + h + 1],
                    in1=gate[:],
                    op0=ALU.add,
                    op1=ALU.mult,
                )
            last_products.append(product)

        def back_group(c, r):
            b = c // 2
            slot = 1 + groups_of(c)[0].start + r
            pool, tag = ((back_pool, "back"), (sums_pool, "sum"))[r]
            back = pool.tile([P, CHUNK_GROUPS, UNITS], F32, name="last_back", tag=tag)
            for h in range(UNIT_TILES):
                nc.tensor.transpose(back[:, 0, h * P : (h + 1) * P], last_products[r][:, h, :], ident[:])
            copy = (nc.scalar.copy, nc.vector.tensor_copy)[r]
            copy(out=result_of[b][:, slot, :], in_=back[:, 0, :])
            nc.sync.dma_start(out=rows_of(out, b)[0][:, slot - 1, :], in_=result_of[b][:, slot, :])

        last_products = []

        def gate_chunk(c):
            product = work.tile([P, UNIT_TILES, CHUNK_ROWS], F32)
            for h in range(UNIT_TILES):
                nc.vector.scalar_tensor_tensor(
                    out=product[:, h, :],
                    in0=sums_of[c][h][:, VALUE, :],
                    scalar=consts["bias"][:, UNIT_TILES + h : UNIT_TILES + h + 1],
                    in1=gates_of[c][h][:],
                    op0=ALU.add,
                    op1=ALU.mult,
                )
            product_of[c] = product

        def store_last(b, n):
            rows = rows_of(out, b)[1][n * P : (n + 1) * P, :].rearrange("(q i) n -> i q n", i=2)
            for i in range(2):
                nc.sync.dma_start(out=rows[i], in_=result_of[b][i * HALF : (i + 1) * HALF, n, :])

        def turn_back_and_store(c):
            b = c // 2
            if c == CHUNKS - 1:
                backs = [
                    back_pool.tile([P, 2, UNITS], F32, name="back%d" % i, tag="back")[:, 0, :]
                    for i in range(CHUNK_GROUPS)
                ]
            else:
                back = back_pool.tile([P, CHUNK_GROUPS, UNITS], F32, tag="back")
                backs = [back[:, i, :] for i in range(CHUNK_GROUPS)]
            for i in range(CHUNK_GROUPS):
                for h in range(UNIT_TILES):
                    nc.tensor.transpose(
                        backs[i][:, h * P : (h + 1) * P],
                        product_of[c][:, h, i * P : (i + 1) * P],
                        ident[:],
                    )
            groups, last_groups = groups_of(c)
            last_count = GROUPS - ADD_GROUPS[b]
            if c % 2 == 0:
                result_of[b] = work.tile([P, GROUPS, UNITS], F32, name="result", bufs=BLOCKS)
            result = result_of[b]
            slots = last_groups + [last_count + group for group in range(groups.start, groups.stop)]
            out_added = rows_of(out, b)[0]
            if b == BLOCKS - 1:
                for i, slot in enumerate(slots):
                    copy = nc.vector.tensor_copy if c == CHUNKS - 1 and i == 1 else nc.scalar.copy
                    copy(out=result[:, slot, :], in_=backs[i])
                    if slot < last_count:
                        store_last(b, slot)
                    else:
                        nc.sync.dma_start(out=out_added[:, slot - last_count, :], in_=result[:, slot, :])
                return
            step = slots[1] - slots[0]
            nc.scalar.copy(out=result[:, slots[0] : slots[1] + 1 : step, :], in_=back[:])
            for n in last_groups:
                store_last(b, n)
            if c % 2 == 1:
                nc.sync.dma_start(out=out_added, in_=result[:, last_count:GROUPS, :])

        ident = const.tile([P, P], F32)
        make_identity(nc, ident[:])

        dt_bf16 = const.tile([P, 1], BF16)
        nc.scalar.dma_start(out=dt_bf16[:], in_=dt.partition_broadcast(P))
        bias_bf16 = const.tile([2 * UNIT_TILES, P], BF16)
        nc.scalar.dma_start(
            out=bias_bf16[0:UNIT_TILES, :], in_=glu_b1.rearrange("(h n) -> h n", n=P)
        )
        nc.scalar.dma_start(
            out=bias_bf16[UNIT_TILES : 2 * UNIT_TILES, :], in_=glu_b2.rearrange("(h n) -> h n", n=P)
        )

        warm = const.tile([P, 2], F32)
        nc.vector.memset(warm[:, 0:1], 0.0)
        nc.scalar.activation(out=warm[:, 1:2], in_=warm[:, 0:1], func=ACT.Sigmoid)

        w_rows = const.tile([P, UNIT_TILES, 2, MODES], BF16)
        w_words = w_rows[:].bitcast(F32)
        w_codes = []
        w_scales = []
        w_grouped = []
        consts = {}

        def load_weights(h):
            for i, weights in enumerate((glu_w1, glu_w2)):
                nc.sync.dma_start(out=w_rows[:, h, i, :], in_=weights[h * P : (h + 1) * P, :])

        def turn_weights(h):
            w_grouped.append(const.tile([P, PASSES, 2 * P, 4], BF16, name="w_grouped%d" % h, align_bytes=64))
            for i in range(2):
                turn(
                    nc,
                    turned_pool,
                    ident,
                    [
                        [w_words[:, h, i, 2 * g * P + u : 2 * (g + 1) * P : 2] for u in range(2)]
                        for g in range(PASSES)
                    ],
                    w_grouped[h][:].bitcast(F32),
                    slice(i * P, (i + 1) * P),
                    nc.scalar.copy,
                )

        def quantise_weights(h):
            w_codes.append(const.tile([P, PASSES, 2 * P], U32, name="w_codes%d" % h, align_bytes=64))
            w_scales.append(const.tile([P, PASSES, 2 * P], U8, name="w_scales%d" % h, align_bytes=64))
            quantise(nc, w_grouped[h], w_codes[h], w_scales[h])

        def make_select():
            dt_part = const.tile([P, HALF], F32, name="dt_part")
            nc.gpsimd.tensor_scalar(
                out=dt_part[:],
                in0=ident[:, 1:P:2],
                scalar1=dt_bf16[:, 0:1],
                scalar2=0.0,
                op0=ALU.mult,
                op1=ALU.add,
            )
            select = const.tile([P, HALF], BF16, name="select")
            nc.gpsimd.tensor_tensor(out=select[:], in0=dt_part[:], in1=ident[:, 0:P:2], op=ALU.add)
            consts["select"] = select

        def lay_biases():
            bias_rows = const.tile([P, P], F32, name="bias_rows")
            nc.vector.memset(bias_rows[:], 0.0)
            nc.vector.tensor_copy(out=bias_rows[0 : 2 * UNIT_TILES, :], in_=bias_bf16[:])
            consts["bias_rows"] = bias_rows

        def turn_biases():
            bias_turned = back_pool.tile([P, CHUNK_GROUPS, UNITS], F32, tag="back")
            nc.tensor.transpose(bias_turned[:, 0, 0:P], consts["bias_rows"][:], ident[:])
            bias_col = const.tile([P, 2 * UNIT_TILES], F32, name="bias_col")
            nc.scalar.copy(out=bias_col[:], in_=bias_turned[:, 0, 0 : 2 * UNIT_TILES])
            consts["bias"] = bias_col

        make_block(0)
        load_added(0, groups_of(0)[0])
        load_last(0, groups_of(0)[1])
        load_weights(0)
        load_weights(1)
        load_added(0, groups_of(1)[0])
        load_last(0, groups_of(1)[1])
        make_block(1)
        load_added(1, groups_of(2)[0])
        load_last(1, groups_of(2)[1])
        load_added(1, groups_of(3)[0])
        for b in range(2, BLOCKS):
            load(b)

        make_select()
        add_chunk(0)
        lay_biases()
        turn_chunk(0)
        turn_weights(0)
        add_chunk(1)
        quantise_weights(0)
        turn_weights(1)
        quantise_weights(1)
        turn_biases()

        for c in range(CHUNKS - 1):
            quantise_chunk(c)
            if c >= 1:
                gate_chunk(c - 1)
            if c + 2 < CHUNKS:
                add_chunk(c + 2)
            turn_chunk(c + 1)
            multiply_chunk(c)
            if c >= 1:
                turn_back_and_store(c - 1)
        c = CHUNKS - 1
        quantise_chunk(c)
        gate_chunk(c - 1)
        multiply_group(c, 0)
        multiply_group(c, 1)
        turn_back_and_store(c - 1)
        back_group(c, 0)
        back_group(c, 1)
